import numpy as np
import ml_dtypes


def mxq(x, axis, fmt="e4m3"):
    dtype, down = {"e4m3": (ml_dtypes.float8_e4m3fn, 7), "e5m2": (ml_dtypes.float8_e5m2, 14)}[fmt]
    v = np.moveaxis(np.asarray(x, np.float32).astype(ml_dtypes.bfloat16).astype(np.float64), axis, -1)
    blocks = v.reshape(v.shape[:-1] + (-1, 32))
    amax = np.abs(blocks).max(-1, keepdims=True)
    byte = np.maximum(np.where(amax > 0, np.frexp(amax)[1] - 1 + 127, 0) - down, 1)
    scale = np.exp2(byte - 127.0)
    codes = (blocks / scale).astype(np.float32).astype(dtype).astype(np.float64)
    return np.moveaxis((codes * scale).reshape(v.shape), -1, axis)


WIDE = False


def mx_kscale(k):
    if not WIDE:
        return np.ones(k)
    levels = np.array([18, -18])
    if k % 512:
        return np.exp2(np.random.permutation(np.resize(levels, k // 32))).repeat(32)
    a = np.empty((k // 512, 16))
    for p in range(k // 512):
        a[p, :8] = np.random.permutation(np.resize(levels, 8))
        for g in range(8):
            far = levels[np.abs(levels - a[p, g]) >= 10]
            a[p, g + 8] = far[np.random.randint(len(far))]
    return np.exp2(a.ravel()).repeat(32)


BF16 = ml_dtypes.bfloat16


def bf(x):
    return np.asarray(x, np.float32).astype(BF16)


def f64(x):
    return np.asarray(x).astype(np.float64)


B, DIM, HID, LS = 512, 128, 512, 23
DL = DIM * LS
O1 = DL
O2 = O1 + DL
O3 = O2 + DL
O4 = O3 + DIM
O5 = O4 + DIM
P = O5 + DIM


def elu(v):
    return np.where(v > 0.0, v, np.exp(np.minimum(v, 0.0)) - 1.0)


def sigmoid(v):
    return 1.0 / (1.0 + np.exp(-v))


def col_scale():
    return np.concatenate([np.full(DL, 0.5), np.full(DL, 1.0), np.full(DL, 2.5 / np.sqrt(LS)),
                           np.full(DIM, 0.5), np.full(DIM, 8.0), np.full(DIM, 2.5)])


def setup_inputs():
    s = mx_kscale(B)[:, None]
    u = mx_kscale(P)[np.arange(DIM) // 32 * (32 * LS)]
    ucol = np.concatenate([np.repeat(u, LS), np.repeat(u, LS), np.repeat(u, LS), u, u, u])
    v = mx_kscale(HID)
    cs = col_scale()
    x = bf(np.random.standard_normal((B, DIM)))
    cond0 = bf(np.random.standard_normal((B, DIM)))
    W1_0 = bf(np.random.standard_normal((DIM, HID)) / np.sqrt(DIM))
    b1 = bf(np.random.standard_normal(HID) * 0.5)
    W2_0 = bf(np.random.standard_normal((HID, P)) * 1.2 / np.sqrt(HID) * cs)
    b2 = bf(np.random.standard_normal(P) * 0.5 * cs)
    g = bf(np.random.standard_normal((B, DIM)) * np.exp2(np.random.randint(-6, 1, (B, 1))) * 8.0 / s * u)
    z1 = f64(cond0) @ f64(W1_0) + f64(b1)
    p = np.maximum(z1, 0.0) @ f64(W2_0) + f64(b2)
    mat1 = p[:, :O1].reshape(B, DIM, LS)
    bias1 = p[:, O1:O2].reshape(B, DIM, LS)
    mat2 = p[:, O2:O3].reshape(B, DIM, LS)
    num = np.sum(elu(f64(x)[:, :, None] * mat1 + bias1) * mat2, axis=-1)
    den = np.sum(np.maximum(-mat1 * mat2, 0.0), axis=-1) + 1.0
    return {"x": x,
            "cond": bf(f64(cond0) * s),
            "W1": bf(f64(W1_0) / v),
            "b1": b1,
            "W2": bf(f64(W2_0) * v[:, None] / ucol),
            "b2": b2,
            "z1": np.asarray(z1, np.float32),
            "p": np.asarray(p, np.float32),
            "num": np.asarray(num, np.float32),
            "den": np.asarray(den, np.float32),
            "grad_out": g}


def reference(x, cond, W1, b1, W2, b2, z1, p, num, den, grad_out):
    x = f64(x)
    p = f64(p)
    num = f64(num)
    den = f64(den)
    g = f64(grad_out)
    n = x.shape[0]
    mat1 = p[:, :O1].reshape(n, DIM, LS)
    bias1 = p[:, O1:O2].reshape(n, DIM, LS)
    mat2 = p[:, O2:O3].reshape(n, DIM, LS)
    eps = p[:, O4:O5] / 10.0
    alpha = p[:, O5:] / 10.0
    sg = sigmoid(eps)
    r = num / den
    t = g * np.exp(alpha)
    deps = 0.08 * t * r * sg * (1.0 - sg)
    dalpha = 0.1 * t * (x + 0.8 * sg * r)
    dnum = 0.8 * t * sg / den
    dden = -dnum * r
    z = x[:, :, None] * mat1 + bias1
    delu = np.where(z > 0.0, 1.0, np.exp(np.minimum(z, 0.0)))
    on = np.where(mat1 * mat2 < 0.0, 1.0, 0.0)
    dbias1 = dnum[:, :, None] * mat2 * delu
    dmat1 = dbias1 * x[:, :, None] - dden[:, :, None] * mat2 * on
    dmat2 = dnum[:, :, None] * elu(z) - dden[:, :, None] * mat1 * on
    dp = np.concatenate([dmat1.reshape(n, DL), dbias1.reshape(n, DL), dmat2.reshape(n, DL), g, deps, dalpha], axis=1)
    dh = mxq(dp, 1, "e5m2") @ mxq(f64(W2), 1, "e4m3").T
    dz1 = dh * np.where(f64(z1) > 0.0, 1.0, 0.0)
    dcond = mxq(dz1, 1, "e5m2") @ mxq(f64(W1), 1, "e4m3").T
    dW1 = mxq(f64(cond), 0, "e4m3").T @ mxq(dz1, 0, "e5m2")
    return dcond, dW1

@@ -1,0 +1,462 @@
+from contextlib import ExitStack
+
+import concourse.mybir as mybir
+from concourse.masks import make_identity
+
+F32 = mybir.dt.float32
+BF16 = mybir.dt.bfloat16
+U32 = mybir.dt.uint32
+U8 = mybir.dt.uint8
+E4M3 = mybir.dt.float8_e4m3fn_x4
+E5M2 = mybir.dt.float8_e5m2_x4
+ALU = mybir.AluOpType
+ACT = mybir.ActivationFunctionType
+
+P = 128
+B, DIM, HID, LS = 512, 128, 512, 23
+J = B // P
+SEC = DIM * LS
+NCOL = 3 * SEC + 3 * DIM
+PASS = 512
+PASSES = NCOL // PASS
+PC = 9216
+
+DC = 32
+CW = DC * LS
+CHUNKS = DIM // DC
+UNITS = J * CHUNKS
+W2_STEPS = 9
+
+FLOPS = 2 * B * NCOL * HID + 2 * 2 * B * HID * DIM
+BYTES = B * (PC - DIM) * 4 + HID * PC * 2 + 3 * B * DIM * 2 + DIM * HID * 2 + B * HID * 4 + 2 * B * DIM * 4 + 2 * B * DIM * 4
+
+
+def chunk_of_column(k):
+    if k < 3 * SEC:
+        return (k % SEC) // CW
+    return 0
+
+
+def pairs_by_chunk():
+    ready = [max(chunk_of_column(k) for k in range(PASS * g, PASS * (g + 1))) for g in range(PASSES)]
+    order = sorted(range(PASSES), key=lambda g: (ready[g], g))
+    pairs = [[] for c in range(CHUNKS)]
+    for s in range(PASSES // 2):
+        a, b = order[2 * s], order[2 * s + 1]
+        pairs[max(ready[a], ready[b])].append((s, a, b))
+    return pairs
+
+
+def tile_cn_pa_v_kernel(tc, x, cond, W1, b1, W2, b2, z1, p, num, den, grad_out, out_0, out_1):
+    nc = tc.nc
+    pairs = pairs_by_chunk()
+    slot_pass = {}
+    for c in range(CHUNKS):
+        for s, a, b in pairs[c]:
+            slot_pass[2 * s] = a
+            slot_pass[2 * s + 1] = b
+    w2_order = [slot_pass[s] for s in range(PASSES)]
+    w2_at = {k: w2_order[k * PASSES // W2_STEPS : (k + 1) * PASSES // W2_STEPS] for k in range(W2_STEPS)}
+
+    def rows(ap):
+        return ap.rearrange("(p j) w -> p j w", j=J)
+
+    with ExitStack() as ctx:
+        keep = ctx.enter_context(tc.tile_pool(name="keep", bufs=1))
+        work = ctx.enter_context(tc.tile_pool(name="work", bufs=2))
+        psum = ctx.enter_context(tc.psum_pool(name="psum", bufs=1))
+
+        ident = keep.tile([P, P], F32, name="ident")
+        make_identity(nc, ident[:])
+        w1q = keep.tile([P, HID], U32, name="w1q", align_bytes=64)
+        w1s = keep.tile([P, HID], U8, name="w1s", align_bytes=64)
+        nc.gpsimd.memset(w1q[:, DIM:], 0)
+        nc.gpsimd.memset(w1s[:, DIM:], 0)
+
+        xb = keep.tile([P, J, DIM], BF16, name="xb")
+        gb = keep.tile([P, J, DIM], BF16, name="gb")
+        rr = keep.tile([P, J, DIM], F32, name="rr")
+        dn = keep.tile([P, J, DIM], F32, name="dn")
+        ea = keep.tile([P, J, 2 * DIM], F32, name="ea")
+        xf = keep.tile([P, J, DIM], F32, name="xf")
+        sg = keep.tile([P, J, DIM], F32, name="sg")
+        om = keep.tile([P, J, DIM], F32, name="om")
+        tt = keep.tile([P, J, DIM], F32, name="tt")
+        dd = keep.tile([P, J, DIM], F32, name="dd")
+        last = keep.tile([P, J, 3 * DIM], BF16, name="last")
+        dp = keep.tile([P, NCOL], BF16, name="dp", align_bytes=64)
+        w2q = keep.tile([P, PASSES, HID], U32, name="w2q", align_bytes=64)
+        w2s = keep.tile([P, PASSES, HID], U8, name="w2s", align_bytes=64)
+        z1t = keep.tile([P, J, HID], F32, name="z1t")
+        dz = keep.tile([P, J, HID], BF16, name="dz", align_bytes=64)
+        w1r = keep.tile([P, HID], BF16, name="w1r", align_bytes=64)
+        w1g = keep.tile([P, HID], BF16, name="w1g", align_bytes=64)
+        cdr = keep.tile([P, J, DIM], BF16, name="cdr")
+        cdg = keep.tile([P, DIM, J], BF16, name="cdg", align_bytes=64)
+        cdq = keep.tile([P, DIM], U32, name="cdq", align_bytes=64)
+        cds = keep.tile([P, DIM], U8, name="cds", align_bytes=64)
+        dzi = keep.tile([P, HID, J], BF16, name="dzi", align_bytes=64)
+        dziq = keep.tile([P, HID], U32, name="dziq", align_bytes=64)
+        dzis = keep.tile([P, HID], U8, name="dzis", align_bytes=64)
+
+        with tc.manual_schedule():
+            tiles = {}
+
+            def load_unit(i):
+                j, c = divmod(i, CHUNKS)
+                src = rows(p)
+                for name, sec, bufs in (("A", 0, 3), ("C", 2, 3), ("B", 1, 4)):
+                    t = work.tile([P, CW], F32, name="pin" + name, bufs=bufs)
+                    nc.sync.dma_start(out=t[:], in_=src[:, j, sec * SEC + c * CW : sec * SEC + (c + 1) * CW])
+                    tiles[name, i] = t
+
+            def load_w2(g):
+                t = work.tile([P, HID // P, PASS], BF16, name="w2r", bufs=2, align_bytes=64)
+                nc.sync.dma_start(out=t[:], in_=W2.rearrange("(h q) k -> q h k", q=P)[:, :, PASS * g : PASS * (g + 1)])
+                tiles["w2r", g] = t
+
+            nc.sync.dma_start(out=xb[:], in_=rows(x))
+            nc.sync.dma_start(out=ea[:], in_=rows(p)[:, :, PC - 2 * DIM :])
+            nc.sync.dma_start(out=dn[:], in_=rows(den))
+            nc.sync.dma_start(out=rr[:], in_=rows(num))
+            nc.sync.dma_start(out=gb[:], in_=rows(grad_out))
+            load_unit(0)
+            load_unit(1)
+            for g in w2_at[0]:
+                load_w2(g)
+
+            def small_a(a, b):
+                v = nc.vector
+                v.reciprocal(dn[:, a:b], dn[:, a:b])
+                v.tensor_tensor(tt[:, a:b], gb[:, a:b], tt[:, a:b], ALU.mult)
+                v.tensor_tensor(rr[:, a:b], rr[:, a:b], dn[:, a:b], ALU.mult)
+                v.tensor_tensor(dn[:, a:b], sg[:, a:b], dn[:, a:b], ALU.mult)
+                v.scalar_tensor_tensor(dd[:, a:b], tt[:, a:b], 0.8, dn[:, a:b], ALU.mult, ALU.mult)
+
+            def small_b(a, b):
+                v = nc.vector
+                c0, c1 = ea[:, a:b, 0:DIM], ea[:, a:b, DIM:]
+                v.tensor_tensor(sg[:, a:b], sg[:, a:b], rr[:, a:b], ALU.mult)
+                v.tensor_copy(last[:, a:b, 0:DIM], gb[:, a:b])
+                v.scalar_tensor_tensor(c0, sg[:, a:b], 0.8, xb[:, a:b], ALU.mult, ALU.add)
+                v.scalar_tensor_tensor(c1, tt[:, a:b], 0.08, sg[:, a:b], ALU.mult, ALU.mult)
+                v.scalar_tensor_tensor(last[:, a:b, 2 * DIM :], tt[:, a:b], 0.1, c0, ALU.mult, ALU.mult)
+                v.tensor_tensor(last[:, a:b, DIM : 2 * DIM], c1, om[:, a:b], ALU.mult)
+
+            def bc(t, i, n0=0, n1=DC):
+                j, c = divmod(i, CHUNKS)
+                return t[:, j, c * DC + n0 : c * DC + n1].unsqueeze(2).to_broadcast([P, n1 - n0, LS])
+
+            def v3(t, n0=0, n1=DC):
+                return t[:, n0 * LS : n1 * LS].rearrange("p (d l) -> p d l", l=LS)
+
+            def dpc(i, sec, n0=0, n1=DC):
+                c = i % CHUNKS
+                o = sec * SEC + c * CW
+                return dp[:, o + n0 * LS : o + n1 * LS]
+
+            def scale_on_scalar(dst, src, t, i, n0, n1):
+                j, c = divmod(i, CHUNKS)
+                for n in range(n0, n1):
+                    d = c * DC + n
+                    nc.scalar.activation(dst[:, (n - n0) * LS : (n - n0 + 1) * LS], src[:, n * LS : (n + 1) * LS], ACT.Copy, scale=t[:, j, d : d + 1])
+
+            def s_m(i):
+                tiles["E", i] = work.tile([P, CW], F32, name="e", bufs=3)
+                scale_on_scalar(tiles["E", i], tiles["A", i], xf, i, 0, DC)
+
+            def s_u(i):
+                tiles["U", i] = work.tile([P, CW], F32, name="u", bufs=2)
+                scale_on_scalar(tiles["U", i], tiles["C", i], dd, i, 0, DC)
+
+            def s_exp(i):
+                e = tiles["E", i]
+                nc.scalar.activation(e[:], tiles["B", i][:], ACT.Relu, scale=-1.0)
+                nc.scalar.activation(e[:], e[:], ACT.Exp, scale=-1.0)
+
+            def v_z(i):
+                nc.vector.tensor_tensor(tiles["B", i][:], tiles["E", i][:], tiles["B", i][:], ALU.add)
+
+            def v_w(i):
+                tiles["W", i] = work.tile([P, CW], F32, name="w", bufs=2)
+                nc.vector.tensor_tensor(tiles["W", i][:], tiles["A", i][:], tiles["C", i][:], ALU.mult)
+
+            def v_q(i):
+                w = tiles["W", i]
+                nc.vector.scalar_tensor_tensor(v3(w), v3(w), 0.0, bc(rr, i), ALU.is_lt, ALU.mult)
+
+            def v_qa(i):
+                tiles["QA", i] = work.tile([P, CW], F32, name="qa", bufs=2)
+                nc.vector.tensor_tensor(tiles["QA", i][:], tiles["W", i][:], tiles["A", i][:], ALU.mult)
+
+            def v_t1(i):
+                tiles["T", i] = work.tile([P, CW], F32, name="t", bufs=1)
+                nc.vector.tensor_tensor(v3(tiles["T", i]), v3(tiles["E", i]), bc(xf, i), ALU.mult)
+
+            def v_t2(i):
+                t = tiles["T", i]
+                nc.vector.tensor_tensor(t[:], t[:], tiles["W", i][:], ALU.add)
+
+            def v_dm1(i):
+                nc.vector.tensor_tensor(dpc(i, 0), tiles["U", i][:], tiles["T", i][:], ALU.mult)
+
+            def v_db1(i):
+                nc.vector.tensor_tensor(dpc(i, 1), tiles["U", i][:], tiles["E", i][:], ALU.mult)
+
+            def v_s1(i):
+                tiles["S", i] = work.tile([P, CW], F32, name="s", bufs=2)
+                nc.vector.scalar_tensor_tensor(tiles["S", i][:], tiles["B", i][:], 0.0, tiles["E", i][:], ALU.max, ALU.add)
+
+            def v_s2(i):
+                s = tiles["S", i]
+                nc.vector.scalar_tensor_tensor(s[:], tiles["QA", i][:], -1.0, s[:], ALU.add, ALU.add)
+
+            def dm2_split(i):
+                return 0
+
+            def v_dm2(i):
+                n = dm2_split(i)
+                if n == 0:
+                    return
+                out = dpc(i, 2, 0, n).rearrange("p (d l) -> p d l", l=LS)
+                nc.vector.tensor_tensor(out, v3(tiles["S", i], 0, n), bc(dd, i, 0, n), ALU.mult)
+
+            def s_dm2(i):
+                n = dm2_split(i)
+                if n < DC:
+                    scale_on_scalar(dpc(i, 2, n, DC), tiles["S", i], dd, i, n, DC)
+
+            def v_last(j):
+                nc.vector.tensor_copy(dp[:, 3 * SEC :], last[:, j, :])
+
+            def turn_dp(j, pair):
+                s, a, b = pair
+                words = dp[:].bitcast(F32)
+                bank = psum.tile([P, 2, 2, P], F32, name="tr", bufs=5)
+                for h, g in enumerate((a, b)):
+                    for u in range(2):
+                        nc.tensor.transpose(bank[:, h, u, :], words[:, 256 * g + u : 256 * (g + 1) : 2], ident[:])
+                grp = work.tile([P, 2 * P * 4], BF16, name="dpg", bufs=4, align_bytes=64)
+                nc.scalar.copy(grp[:].bitcast(F32).rearrange("p (h r u) -> p h r u", h=2, u=2), bank[:].rearrange("p h u r -> p h r u"))
+
+                def quant():
+                    if ("dpq", j) not in tiles:
+                        tiles["dpq", j] = work.tile([P, PASSES * P], U32, name="dpq", bufs=2, align_bytes=64)
+                        tiles["dps", j] = work.tile([P, PASSES * P], U8, name="dps", bufs=2, align_bytes=64)
+                    cols = slice(2 * s * P, (2 * s + 2) * P)
+                    nc.vector.quantize_mx(out=tiles["dpq", j][:, cols].bitcast(E5M2), scales=tiles["dps", j][:, cols], in_=grp[:])
+                    mx_ready.append((j, 2 * s))
+                    mx_ready.append((j, 2 * s + 1))
+
+                return quant
+
+            def turn_w2(g):
+                words = tiles["w2r", g][:].bitcast(F32)
+                grp = work.tile([P, HID * 4], BF16, name="w2g", bufs=2, align_bytes=64)
+                for half in range(2):
+                    bank = psum.tile([P, 2, 2, P], F32, name="tr", bufs=5)
+                    for h in range(2):
+                        for u in range(2):
+                            nc.tensor.transpose(bank[:, h, u, :], words[:, 2 * half + h, u:256:2], ident[:])
+                    out = grp[:].bitcast(F32)[:, 512 * half : 512 * (half + 1)].rearrange("p (h r u) -> p h r u", h=2, u=2)
+                    nc.scalar.copy(out, bank[:].rearrange("p h u r -> p h r u"))
+
+                def quant():
+                    nc.vector.quantize_mx(out=w2q[:, g, :].bitcast(E4M3), scales=w2s[:, g, :], in_=grp[:])
+                    w2_done.append(g)
+
+                return quant
+
+            mx_ready = []
+            w2_done = []
+
+            def mx(j, s):
+                if ("acc", j) not in tiles:
+                    tiles["acc", j] = psum.tile([P, HID], F32, name="acc", bufs=3)
+                    tiles["n", j] = 0
+                g = slot_pass[s]
+                n = tiles["n", j]
+                nc.tensor.matmul_mx(
+                    out=tiles["acc", j][:],
+                    lhsT=tiles["dpq", j][:, s * P : (s + 1) * P].bitcast(E5M2),
+                    lhsT_scale=tiles["dps", j][:, s * P : (s + 1) * P],
+                    rhs=w2q[:, g, :].bitcast(E4M3),
+                    rhs_scale=w2s[:, g, :],
+                    start=(n == 0),
+                    stop=(n == PASSES - 1),
+                )
+                tiles["n", j] = n + 1
+                return n == PASSES - 1
+
+            def dz_mask(j):
+                nc.vector.scalar_tensor_tensor(dz[:, j, :], z1t[:, j, :], 0.0, tiles["acc", j][:], ALU.is_gt, ALU.mult)
+
+            def dz_turn(j):
+                words = dz[:, j, :].bitcast(F32)
+                bank = psum.tile([P, 2, P], F32, name="tr", bufs=5)
+                for u in range(2):
+                    nc.tensor.transpose(bank[:, u, :], words[:, u:256:2], ident[:])
+                grp = work.tile([P, P * 4], BF16, name="dzg", bufs=2, align_bytes=64)
+                nc.scalar.copy(grp[:].bitcast(F32).rearrange("p (r u) -> p r u", u=2), bank[:].rearrange("p u r -> p r u"))
+
+                def quant():
+                    q = work.tile([P, P], U32, name="dzq", bufs=2, align_bytes=64)
+                    sc = work.tile([P, P], U8, name="dzs", bufs=2, align_bytes=64)
+                    nc.vector.quantize_mx(out=q[:].bitcast(E5M2), scales=sc[:], in_=grp[:])
+                    tiles["dzq", j] = (q, sc)
+
+                return quant
+
+            def dz_mx(j):
+                q, sc = tiles["dzq", j]
+                o = psum.tile([P, HID], F32, name="acc", bufs=3)
+                nc.tensor.matmul_mx(out=o[:], lhsT=q[:].bitcast(E5M2), lhsT_scale=sc[:], rhs=w1q[:].bitcast(E4M3), rhs_scale=w1s[:], start=True, stop=True)
+                tiles["o", j] = o
+
+            def dz_store(j):
+                ob = work.tile([P, DIM], F32, name="ob", bufs=2)
+                nc.scalar.copy(ob[:], tiles["o", j][:, 0:DIM])
+                nc.sync.dma_start(out=rows(out_0)[:, j, :], in_=ob[:])
+
+            def w1_turn():
+                words = w1r[:].bitcast(F32)
+                bank = psum.tile([P, 2, P], F32, name="tr", bufs=5)
+                for u in range(2):
+                    nc.tensor.transpose(bank[:, u, :], words[:, u:256:2], ident[:])
+                nc.scalar.copy(w1g[:].bitcast(F32).rearrange("p (r u) -> p r u", u=2), bank[:].rearrange("p u r -> p r u"))
+
+            def w1_quant():
+                nc.vector.quantize_mx(out=w1q[:, 0:DIM].bitcast(E4M3), scales=w1s[:, 0:DIM], in_=w1g[:])
+
+            def cond_group():
+                nc.vector.tensor_copy(cdg[:], cdr[:].rearrange("p j d -> p d j"))
+
+            def cond_quant():
+                nc.vector.quantize_mx(out=cdq[:].bitcast(E4M3), scales=cds[:], in_=cdg[:].rearrange("p d j -> p (d j)"))
+
+            nc.scalar.activation(sg[:], ea[:, :, 0:DIM], ACT.Sigmoid, scale=0.1)
+            nc.scalar.activation(om[:], ea[:, :, 0:DIM], ACT.Sigmoid, scale=-0.1)
+            nc.scalar.activation(tt[:], ea[:, :, DIM:], ACT.Exp, scale=0.1)
+            nc.vector.tensor_copy(xf[:], xb[:])
+            s_m(0)
+            small_a(0, 1)
+
+            pend = []
+            stage = {}
+            for k in range(-1, UNITS + 1):
+                new = []
+                if k >= 1:
+                    s_dm2(k - 1)
+                nxt = k + 1 < UNITS
+                cur = 0 <= k < UNITS
+                if nxt:
+                    v_z(k + 1)
+                    s_exp(k + 1)
+                if k >= 1:
+                    j, c = divmod(k - 1, CHUNKS)
+                    for pair in pairs[c]:
+                        new.append(turn_dp(j, pair))
+                if k + 2 < UNITS:
+                    s_m(k + 2)
+                for g in w2_at.get(k, []):
+                    new.append(turn_w2(g))
+                if k == 2:
+                    w1_turn()
+                    new.append(w1_quant)
+                    new.append(cond_group)
+                    new.append(cond_quant)
+                for j in range(J):
+                    if stage.get(j) == (k - 1, "mask"):
+                        new.append(dz_turn(j))
+                        stage[j] = (k, "turn")
+                    elif stage.get(j) == (k - 1, "mx"):
+                        dz_store(j)
+                        stage[j] = (k, "store")
+                if nxt:
+                    s_u(k + 1)
+
+                todo = []
+                if cur:
+                    todo.append(lambda: v_t1(k))
+                if nxt:
+                    todo.append(lambda: v_w(k + 1))
+                if cur:
+                    todo.append(lambda: v_t2(k))
+                if nxt:
+                    todo.append(lambda: v_q(k + 1))
+                if cur:
+                    todo.append(lambda: v_dm1(k))
+                    todo.append(lambda: v_s1(k))
+                if nxt:
+                    todo.append(lambda: v_qa(k + 1))
+                if cur:
+                    todo.append(lambda: v_s2(k))
+                    todo.append(lambda: v_db1(k))
+                    todo.append(lambda: v_dm2(k))
+                if cur and k % CHUNKS == 1:
+                    todo.append(lambda: v_last(k // CHUNKS))
+                if k == -1:
+                    todo.append(lambda: small_a(1, J))
+                if k == 0:
+                    todo.append(lambda: small_b(0, J))
+                w2_was = len(w2_done)
+                ready_now = len(mx_ready)
+                n = max(len(todo), 1)
+                done = 0
+                for m in range(n):
+                    if m < len(todo):
+                        todo[m]()
+                    want = len(pend) * (m + 1) // n
+                    while done < want:
+                        pend[done]()
+                        done += 1
+                pend = new
+
+                if k + 3 < UNITS:
+                    load_unit(k + 3)
+                for g in w2_at.get(k + 1, []) if k >= 0 else []:
+                    load_w2(g)
+                if k == 0:
+                    nc.sync.dma_start(out=w1r[:], in_=W1)
+                    nc.sync.dma_start(out=cdr[:], in_=rows(cond))
+                if k == 5:
+                    nc.sync.dma_start(out=z1t[:], in_=rows(z1))
+
+                for j in range(J):
+                    if stage.get(j) == (k - 1, "turn"):
+                        dz_mx(j)
+                        stage[j] = (k, "mx")
+                if len(w2_done) == PASSES:
+                    take = min(ready_now, PASSES)
+                    for j, s in mx_ready[:take]:
+                        if mx(j, s):
+                            pend.append(lambda j=j: dz_mask(j))
+                            stage[j] = (k + 1, "mask")
+                    mx_ready = mx_ready[take:]
+
+            for task in pend:
+                task()
+            for j, s in mx_ready:
+                mx(j, s)
+            for j in range(J):
+                if j not in stage:
+                    dz_mask(j)
+                    dz_turn(j)()
+                    dz_mx(j)
+                    dz_store(j)
+                elif stage[j][1] == "mask":
+                    dz_turn(j)()
+                    dz_mx(j)
+                    dz_store(j)
+                elif stage[j][1] == "turn":
+                    dz_mx(j)
+                    dz_store(j)
+                elif stage[j][1] == "mx":
+                    dz_store(j)
+            nc.vector.tensor_copy(dzi[:], dz[:].rearrange("p j h -> p h j"))
+            nc.vector.quantize_mx(out=dziq[:].bitcast(E5M2), scales=dzis[:], in_=dzi[:].rearrange("p h j -> p (h j)"))
+            o1 = psum.tile([P, HID], F32, name="acc", bufs=3)
+            nc.tensor.matmul_mx(out=o1[:], lhsT=cdq[:].bitcast(E4M3), lhsT_scale=cds[:], rhs=dziq[:].bitcast(E5M2), rhs_scale=dzis[:], start=True, stop=True)
+            ob1 = work.tile([P, HID], F32, name="ob1", bufs=1)
+            nc.scalar.copy(ob1[:], o1[:])
+            nc.sync.dma_start(out=out_1, in_=ob1[:])

@@ -21,42 +21,45 @@ PASS = 512
 PASSES = NCOL // PASS
 PC = 9216
 
-DC = 32
-CW = DC * LS
-CHUNKS = DIM // DC
-UNITS = J * CHUNKS
-W2_STEPS = 9
+SIZES = [[8, 24, 32, 32, 32], [32, 32, 32, 32], [32, 32, 32, 32], [32, 32, 32, 24, 8]]
+CW = max(max(s) for s in SIZES) * LS
+UNITS = [(j, sum(SIZES[j][:c]), n) for j in range(J) for c, n in enumerate(SIZES[j])]
+NU = len(UNITS)
+W2_STEPS = 10
+ADD_ON_TENSOR = range(4, 14)
+T1_ON_SCALAR = 3
 
 FLOPS = 2 * B * NCOL * HID + 2 * 2 * B * HID * DIM
 BYTES = B * (PC - DIM) * 4 + HID * PC * 2 + 3 * B * DIM * 2 + DIM * HID * 2 + B * HID * 4 + 2 * B * DIM * 4 + 2 * B * DIM * 4
 
 
-def chunk_of_column(k):
-    if k < 3 * SEC:
-        return (k % SEC) // CW
-    return 0
+def pairs_by_unit():
+    result = []
+    for j in range(J):
+        ends = [sum(SIZES[j][: c + 1]) * LS for c in range(len(SIZES[j]))]
 
+        def chunk(k):
+            return min(c for c in range(len(ends)) if k % SEC < ends[c]) if k < 3 * SEC else 0
 
-def pairs_by_chunk():
-    ready = [max(chunk_of_column(k) for k in range(PASS * g, PASS * (g + 1))) for g in range(PASSES)]
-    order = sorted(range(PASSES), key=lambda g: (ready[g], g))
-    pairs = [[] for c in range(CHUNKS)]
-    for s in range(PASSES // 2):
-        a, b = order[2 * s], order[2 * s + 1]
-        pairs[max(ready[a], ready[b])].append((s, a, b))
-    return pairs
+        ready = [max(chunk(k) for k in range(PASS * g, PASS * (g + 1))) for g in range(PASSES)]
+        order = sorted(range(PASSES), key=lambda g: (ready[g], g))
+        pairs = [[] for c in ends]
+        for s in range(PASSES // 2):
+            a, b = order[2 * s], order[2 * s + 1]
+            pairs[max(ready[a], ready[b])].append((s, a, b))
+        result.extend(pairs)
+    return result
 
 
 def tile_cn_pa_v_kernel(tc, x, cond, W1, b1, W2, b2, z1, p, num, den, grad_out, out_0, out_1):
     nc = tc.nc
-    pairs = pairs_by_chunk()
+    pairs = pairs_by_unit()
     slot_pass = {}
-    for c in range(CHUNKS):
-        for s, a, b in pairs[c]:
-            slot_pass[2 * s] = a
-            slot_pass[2 * s + 1] = b
-    w2_order = [slot_pass[s] for s in range(PASSES)]
-    w2_at = {k: w2_order[k * PASSES // W2_STEPS : (k + 1) * PASSES // W2_STEPS] for k in range(W2_STEPS)}
+    for i, (j, d0, n) in enumerate(UNITS):
+        for s, a, b in pairs[i]:
+            slot_pass[j, 2 * s] = a
+            slot_pass[j, 2 * s + 1] = b
+    w2_at = {k: range(k * PASSES // W2_STEPS, (k + 1) * PASSES // W2_STEPS) for k in range(W2_STEPS)}
 
     def rows(ap):
         return ap.rearrange("(p j) w -> p j w", j=J)
@@ -103,12 +106,11 @@ def tile_cn_pa_v_kernel(tc, x, cond, W1, b1, W2, b2, z1, p, num, den, grad_out, 
             tiles = {}
 
             def load_unit(i):
-                j, c = divmod(i, CHUNKS)
-                src = rows(p)
-                for name, sec, bufs in (("A", 0, 3), ("C", 2, 3), ("B", 1, 4)):
+                j, d0, n = UNITS[i]
+                for name, sec, bufs in (("A", 0, 3), ("C", 2, 4), ("B", 1, 4)):
                     t = work.tile([P, CW], F32, name="pin" + name, bufs=bufs)
-                    nc.sync.dma_start(out=t[:], in_=src[:, j, sec * SEC + c * CW : sec * SEC + (c + 1) * CW])
-                    tiles[name, i] = t
+                    nc.sync.dma_start(out=t[:, : n * LS], in_=rows(p)[:, j, sec * SEC + d0 * LS : sec * SEC + (d0 + n) * LS])
+                    tiles[name, i] = t[:, : n * LS]
 
             def load_w2(g):
                 t = work.tile([P, HID // P, PASS], BF16, name="w2r", bufs=2, align_bytes=64)
@@ -116,11 +118,11 @@ def tile_cn_pa_v_kernel(tc, x, cond, W1, b1, W2, b2, z1, p, num, den, grad_out, 
                 tiles["w2r", g] = t
 
             nc.sync.dma_start(out=xb[:], in_=rows(x))
-            nc.sync.dma_start(out=ea[:], in_=rows(p)[:, :, PC - 2 * DIM :])
+            load_unit(0)
             nc.sync.dma_start(out=dn[:], in_=rows(den))
             nc.sync.dma_start(out=rr[:], in_=rows(num))
+            nc.sync.dma_start(out=ea[:], in_=rows(p)[:, :, PC - 2 * DIM :])
             nc.sync.dma_start(out=gb[:], in_=rows(grad_out))
-            load_unit(0)
             load_unit(1)
             for g in w2_at[0]:
                 load_w2(g)
@@ -143,101 +145,119 @@ def tile_cn_pa_v_kernel(tc, x, cond, W1, b1, W2, b2, z1, p, num, den, grad_out, 
                 v.scalar_tensor_tensor(last[:, a:b, 2 * DIM :], tt[:, a:b], 0.1, c0, ALU.mult, ALU.mult)
                 v.tensor_tensor(last[:, a:b, DIM : 2 * DIM], c1, om[:, a:b], ALU.mult)
 
-            def bc(t, i, n0=0, n1=DC):
-                j, c = divmod(i, CHUNKS)
-                return t[:, j, c * DC + n0 : c * DC + n1].unsqueeze(2).to_broadcast([P, n1 - n0, LS])
+            def bc(t, i, n=None):
+                j, d0, size = UNITS[i]
+                n = size if n is None else n
+                return t[:, j, d0 : d0 + n].unsqueeze(2).to_broadcast([P, n, LS])
 
-            def v3(t, n0=0, n1=DC):
-                return t[:, n0 * LS : n1 * LS].rearrange("p (d l) -> p d l", l=LS)
+            def v3(t):
+                return t.rearrange("p (d l) -> p d l", l=LS)
 
-            def dpc(i, sec, n0=0, n1=DC):
-                c = i % CHUNKS
-                o = sec * SEC + c * CW
-                return dp[:, o + n0 * LS : o + n1 * LS]
-
-            def scale_on_scalar(dst, src, t, i, n0, n1):
-                j, c = divmod(i, CHUNKS)
-                for n in range(n0, n1):
-                    d = c * DC + n
-                    nc.scalar.activation(dst[:, (n - n0) * LS : (n - n0 + 1) * LS], src[:, n * LS : (n + 1) * LS], ACT.Copy, scale=t[:, j, d : d + 1])
+            def new_tile(key, i, bufs):
+                tiles[key, i] = work.tile([P, CW], F32, name="t" + key, bufs=bufs)[:, : UNITS[i][2] * LS]
+                return tiles[key, i]
 
             def s_m(i):
-                tiles["E", i] = work.tile([P, CW], F32, name="e", bufs=3)
-                scale_on_scalar(tiles["E", i], tiles["A", i], xf, i, 0, DC)
+                j, d0, n = UNITS[i]
+                m = new_tile("E", i, 3)
+                for d in range(n):
+                    run = slice(d * LS, (d + 1) * LS)
+                    nc.scalar.activation(m[:, run], tiles["A", i][:, run], ACT.Copy, scale=xf[:, j, d0 + d : d0 + d + 1])
 
-            def s_u(i):
-                tiles["U", i] = work.tile([P, CW], F32, name="u", bufs=2)
-                scale_on_scalar(tiles["U", i], tiles["C", i], dd, i, 0, DC)
+            def s_out(i):
+                j, d0, n = UNITS[i]
+                out = dp[:, : 3 * SEC].rearrange("p (s w) -> p s w", s=3)
+                for d in range(n):
+                    nc.scalar.activation(
+                        out[:, :, (d0 + d) * LS : (d0 + d + 1) * LS],
+                        tiles["Y", i][:, :, d * LS : (d + 1) * LS],
+                        ACT.Copy,
+                        scale=dd[:, j, d0 + d : d0 + d + 1],
+                    )
 
             def s_exp(i):
                 e = tiles["E", i]
-                nc.scalar.activation(e[:], tiles["B", i][:], ACT.Relu, scale=-1.0)
-                nc.scalar.activation(e[:], e[:], ACT.Exp, scale=-1.0)
+                nc.scalar.activation(e, tiles["B", i], ACT.Relu, scale=-1.0)
+                nc.scalar.activation(e, e, ACT.Exp, scale=-1.0)
+
+            def y(i, s):
+                return tiles["Y", i][:, s, : UNITS[i][2] * LS]
 
             def v_z(i):
-                nc.vector.tensor_tensor(tiles["B", i][:], tiles["E", i][:], tiles["B", i][:], ALU.add)
+                nc.vector.tensor_tensor(tiles["B", i], tiles["E", i], tiles["B", i], ALU.add)
 
             def v_w(i):
-                tiles["W", i] = work.tile([P, CW], F32, name="w", bufs=2)
-                nc.vector.tensor_tensor(tiles["W", i][:], tiles["A", i][:], tiles["C", i][:], ALU.mult)
+                nc.vector.tensor_tensor(new_tile("W", i, 2), tiles["A", i], tiles["C", i], ALU.mult)
 
             def v_q(i):
-                w = tiles["W", i]
-                nc.vector.scalar_tensor_tensor(v3(w), v3(w), 0.0, bc(rr, i), ALU.is_lt, ALU.mult)
+                w = v3(tiles["W", i])
+                nc.vector.scalar_tensor_tensor(w, w, 0.0, bc(rr, i), ALU.is_lt, ALU.mult)
 
             def v_qa(i):
-                tiles["QA", i] = work.tile([P, CW], F32, name="qa", bufs=2)
-                nc.vector.tensor_tensor(tiles["QA", i][:], tiles["W", i][:], tiles["A", i][:], ALU.mult)
+                nc.vector.tensor_tensor(new_tile("QA", i, 2), tiles["W", i], tiles["A", i], ALU.mult)
+
+            def t1_scalar(i):
+                return UNITS[i][2] * T1_ON_SCALAR // 8
+
+            def s_t1(i):
+                yt = work.tile([P, 3, CW], F32, name="yt", bufs=2)
+                tiles["Y", i] = yt
+                j, d0, n = UNITS[i]
+                for d in range(n - t1_scalar(i), n):
+                    run = slice(d * LS, (d + 1) * LS)
+                    nc.scalar.activation(y(i, 0)[:, run], tiles["E", i][:, run], ACT.Copy, scale=xf[:, j, d0 + d : d0 + d + 1])
 
             def v_t1(i):
-                tiles["T", i] = work.tile([P, CW], F32, name="t", bufs=1)
-                nc.vector.tensor_tensor(v3(tiles["T", i]), v3(tiles["E", i]), bc(xf, i), ALU.mult)
+                n = UNITS[i][2] - t1_scalar(i)
+                nc.vector.tensor_tensor(v3(y(i, 0)[:, : n * LS]), v3(tiles["E", i][:, : n * LS]), bc(xf, i, n), ALU.mult)
+
+            def pe_t2(i):
+                half = UNITS[i][2] * LS // 2
+                tiles["t2", i] = psum.tile([P, 2, HID], F32, name="t2", bufs=1)
+                for h in range(2):
+                    cols = slice(h * half, (h + 1) * half)
+                    out = tiles["t2", i][:, h, :half]
+                    nc.tensor.matmul(out, lhsT=ident[:], rhs=y(i, 0)[:, cols], start=True, stop=False)
+                    nc.tensor.matmul(out, lhsT=ident[:], rhs=tiles["W", i][:, cols], start=False, stop=True)
 
             def v_t2(i):
-                t = tiles["T", i]
-                nc.vector.tensor_tensor(t[:], t[:], tiles["W", i][:], ALU.add)
+                nc.vector.tensor_tensor(y(i, 0), y(i, 0), tiles["W", i], ALU.add)
 
-            def v_dm1(i):
-                nc.vector.tensor_tensor(dpc(i, 0), tiles["U", i][:], tiles["T", i][:], ALU.mult)
+            def v_y1_psum(i, h):
+                half = UNITS[i][2] * LS // 2
+                cols = slice(h * half, (h + 1) * half)
+                nc.vector.tensor_tensor(y(i, 0)[:, cols], tiles["t2", i][:, h, :half], tiles["C", i][:, cols], ALU.mult)
 
-            def v_db1(i):
-                nc.vector.tensor_tensor(dpc(i, 1), tiles["U", i][:], tiles["E", i][:], ALU.mult)
+            def v_y1(i):
+                nc.vector.tensor_tensor(y(i, 0), y(i, 0), tiles["C", i], ALU.mult)
+
+            def v_y2(i):
+                nc.vector.tensor_tensor(y(i, 1), tiles["E", i], tiles["C", i], ALU.mult)
 
             def v_s1(i):
-                tiles["S", i] = work.tile([P, CW], F32, name="s", bufs=2)
-                nc.vector.scalar_tensor_tensor(tiles["S", i][:], tiles["B", i][:], 0.0, tiles["E", i][:], ALU.max, ALU.add)
+                nc.vector.scalar_tensor_tensor(y(i, 2), tiles["B", i], 0.0, tiles["E", i], ALU.max, ALU.add)
 
             def v_s2(i):
-                s = tiles["S", i]
-                nc.vector.scalar_tensor_tensor(s[:], tiles["QA", i][:], -1.0, s[:], ALU.add, ALU.add)
-
-            def dm2_split(i):
-                return 0
-
-            def v_dm2(i):
-                n = dm2_split(i)
-                if n == 0:
-                    return
-                out = dpc(i, 2, 0, n).rearrange("p (d l) -> p d l", l=LS)
-                nc.vector.tensor_tensor(out, v3(tiles["S", i], 0, n), bc(dd, i, 0, n), ALU.mult)
-
-            def s_dm2(i):
-                n = dm2_split(i)
-                if n < DC:
-                    scale_on_scalar(dpc(i, 2, n, DC), tiles["S", i], dd, i, n, DC)
+                nc.vector.scalar_tensor_tensor(y(i, 2), tiles["QA", i], -1.0, y(i, 2), ALU.add, ALU.add)
 
             def v_last(j):
                 nc.vector.tensor_copy(dp[:, 3 * SEC :], last[:, j, :])
 
-            def turn_dp(j, pair):
+            def copy_words(engine, out, bank):
+                if engine == "vector":
+                    nc.vector.tensor_copy(out, bank)
+                else:
+                    nc.scalar.copy(out, bank)
+
+            def turn_dp(j, pair, engine="scalar"):
                 s, a, b = pair
                 words = dp[:].bitcast(F32)
-                bank = psum.tile([P, 2, 2, P], F32, name="tr", bufs=5)
+                bank = psum.tile([P, 2, 2, P], F32, name="tr", bufs=4)
                 for h, g in enumerate((a, b)):
                     for u in range(2):
                         nc.tensor.transpose(bank[:, h, u, :], words[:, 256 * g + u : 256 * (g + 1) : 2], ident[:])
                 grp = work.tile([P, 2 * P * 4], BF16, name="dpg", bufs=4, align_bytes=64)
-                nc.scalar.copy(grp[:].bitcast(F32).rearrange("p (h r u) -> p h r u", h=2, u=2), bank[:].rearrange("p h u r -> p h r u"))
+                copy_words(engine, grp[:].bitcast(F32).rearrange("p (h r u) -> p h r u", h=2, u=2), bank[:].rearrange("p h u r -> p h r u"))
 
                 def quant():
                     if ("dpq", j) not in tiles:
@@ -254,7 +274,7 @@ def tile_cn_pa_v_kernel(tc, x, cond, W1, b1, W2, b2, z1, p, num, den, grad_out, 
                 words = tiles["w2r", g][:].bitcast(F32)
                 grp = work.tile([P, HID * 4], BF16, name="w2g", bufs=2, align_bytes=64)
                 for half in range(2):
-                    bank = psum.tile([P, 2, 2, P], F32, name="tr", bufs=5)
+                    bank = psum.tile([P, 2, 2, P], F32, name="tr", bufs=4)
                     for h in range(2):
                         for u in range(2):
                             nc.tensor.transpose(bank[:, h, u, :], words[:, 2 * half + h, u:256:2], ident[:])
@@ -272,9 +292,9 @@ def tile_cn_pa_v_kernel(tc, x, cond, W1, b1, W2, b2, z1, p, num, den, grad_out, 
 
             def mx(j, s):
                 if ("acc", j) not in tiles:
-                    tiles["acc", j] = psum.tile([P, HID], F32, name="acc", bufs=3)
+                    tiles["acc", j] = psum.tile([P, HID], F32, name="acc", bufs=2)
                     tiles["n", j] = 0
-                g = slot_pass[s]
+                g = slot_pass[j, s]
                 n = tiles["n", j]
                 nc.tensor.matmul_mx(
                     out=tiles["acc", j][:],
@@ -293,7 +313,7 @@ def tile_cn_pa_v_kernel(tc, x, cond, W1, b1, W2, b2, z1, p, num, den, grad_out, 
 
             def dz_turn(j):
                 words = dz[:, j, :].bitcast(F32)
-                bank = psum.tile([P, 2, P], F32, name="tr", bufs=5)
+                bank = psum.tile([P, 2, P], F32, name="tr", bufs=4)
                 for u in range(2):
                     nc.tensor.transpose(bank[:, u, :], words[:, u:256:2], ident[:])
                 grp = work.tile([P, P * 4], BF16, name="dzg", bufs=2, align_bytes=64)
@@ -309,7 +329,7 @@ def tile_cn_pa_v_kernel(tc, x, cond, W1, b1, W2, b2, z1, p, num, den, grad_out, 
 
             def dz_mx(j):
                 q, sc = tiles["dzq", j]
-                o = psum.tile([P, HID], F32, name="acc", bufs=3)
+                o = psum.tile([P, HID], F32, name="acc", bufs=2)
                 nc.tensor.matmul_mx(out=o[:], lhsT=q[:].bitcast(E5M2), lhsT_scale=sc[:], rhs=w1q[:].bitcast(E4M3), rhs_scale=w1s[:], start=True, stop=True)
                 tiles["o", j] = o
 
@@ -320,7 +340,7 @@ def tile_cn_pa_v_kernel(tc, x, cond, W1, b1, W2, b2, z1, p, num, den, grad_out, 
 
             def w1_turn():
                 words = w1r[:].bitcast(F32)
-                bank = psum.tile([P, 2, P], F32, name="tr", bufs=5)
+                bank = psum.tile([P, 2, P], F32, name="tr", bufs=4)
                 for u in range(2):
                     nc.tensor.transpose(bank[:, u, :], words[:, u:256:2], ident[:])
                 nc.scalar.copy(w1g[:].bitcast(F32).rearrange("p (r u) -> p r u", u=2), bank[:].rearrange("p u r -> p r u"))
@@ -334,29 +354,35 @@ def tile_cn_pa_v_kernel(tc, x, cond, W1, b1, W2, b2, z1, p, num, den, grad_out, 
             def cond_quant():
                 nc.vector.quantize_mx(out=cdq[:].bitcast(E4M3), scales=cds[:], in_=cdg[:].rearrange("p d j -> p (d j)"))
 
+            nc.vector.memset(sg[:, 0, 0:1], 0.0)
+            nc.scalar.activation(sg[:, 0, 0:1], sg[:, 0, 0:1], ACT.Sigmoid)
+            nc.vector.tensor_copy(xf[:], xb[:])
+            s_m(0)
             nc.scalar.activation(sg[:], ea[:, :, 0:DIM], ACT.Sigmoid, scale=0.1)
             nc.scalar.activation(om[:], ea[:, :, 0:DIM], ACT.Sigmoid, scale=-0.1)
             nc.scalar.activation(tt[:], ea[:, :, DIM:], ACT.Exp, scale=0.1)
-            nc.vector.tensor_copy(xf[:], xb[:])
-            s_m(0)
-            small_a(0, 1)
 
             pend = []
             stage = {}
-            for k in range(-1, UNITS + 1):
+            for k in range(-1, NU):
                 new = []
+                nxt = k + 1 < NU
+                cur = k >= 0
+                if cur:
+                    s_t1(k)
                 if k >= 1:
-                    s_dm2(k - 1)
-                nxt = k + 1 < UNITS
-                cur = 0 <= k < UNITS
+                    s_out(k - 1)
                 if nxt:
                     v_z(k + 1)
                     s_exp(k + 1)
+                if cur:
+                    v_t1(k)
+                if k in ADD_ON_TENSOR:
+                    pe_t2(k)
                 if k >= 1:
-                    j, c = divmod(k - 1, CHUNKS)
-                    for pair in pairs[c]:
-                        new.append(turn_dp(j, pair))
-                if k + 2 < UNITS:
+                    for pair in pairs[k - 1]:
+                        new.append(turn_dp(UNITS[k - 1][0], pair))
+                if k + 2 < NU:
                     s_m(k + 2)
                 for g in w2_at.get(k, []):
                     new.append(turn_w2(g))
@@ -372,33 +398,20 @@ def tile_cn_pa_v_kernel(tc, x, cond, W1, b1, W2, b2, z1, p, num, den, grad_out, 
                     elif stage.get(j) == (k - 1, "mx"):
                         dz_store(j)
                         stage[j] = (k, "store")
-                if nxt:
-                    s_u(k + 1)
 
                 todo = []
-                if cur:
-                    todo.append(lambda: v_t1(k))
-                if nxt:
-                    todo.append(lambda: v_w(k + 1))
-                if cur:
-                    todo.append(lambda: v_t2(k))
-                if nxt:
-                    todo.append(lambda: v_q(k + 1))
-                if cur:
-                    todo.append(lambda: v_dm1(k))
-                    todo.append(lambda: v_s1(k))
-                if nxt:
-                    todo.append(lambda: v_qa(k + 1))
-                if cur:
-                    todo.append(lambda: v_s2(k))
-                    todo.append(lambda: v_db1(k))
-                    todo.append(lambda: v_dm2(k))
-                if cur and k % CHUNKS == 1:
-                    todo.append(lambda: v_last(k // CHUNKS))
                 if k == -1:
-                    todo.append(lambda: small_a(1, J))
-                if k == 0:
-                    todo.append(lambda: small_b(0, J))
+                    todo += [lambda: v_w(0), lambda: small_a(0, J), lambda: v_q(0), lambda: v_qa(0), lambda: small_b(0, J)]
+                else:
+                    second = [lambda: v_w(k + 1), lambda: v_q(k + 1), lambda: v_qa(k + 1)] if nxt else []
+                    if k in ADD_ON_TENSOR:
+                        todo += second[:1] + [lambda: v_s1(k)] + second[1:2] + [lambda: v_y2(k), lambda: v_s2(k)] + second[2:]
+                        todo += [lambda: v_y1_psum(k, 0), lambda: v_y1_psum(k, 1)]
+                    else:
+                        todo += second[:1] + [lambda: v_t2(k)] + second[1:2] + [lambda: v_s1(k), lambda: v_y1(k)] + second[2:]
+                        todo += [lambda: v_s2(k), lambda: v_y2(k)]
+                if cur and UNITS[k][1] == SIZES[UNITS[k][0]][0]:
+                    todo.append(lambda: v_last(UNITS[k][0]))
                 w2_was = len(w2_done)
                 ready_now = len(mx_ready)
                 n = max(len(todo), 1)
@@ -412,14 +425,14 @@ def tile_cn_pa_v_kernel(tc, x, cond, W1, b1, W2, b2, z1, p, num, den, grad_out, 
                         done += 1
                 pend = new
 
-                if k + 3 < UNITS:
+                if k + 3 < NU:
                     load_unit(k + 3)
                 for g in w2_at.get(k + 1, []) if k >= 0 else []:
                     load_w2(g)
                 if k == 0:
                     nc.sync.dma_start(out=w1r[:], in_=W1)
                     nc.sync.dma_start(out=cdr[:], in_=rows(cond))
-                if k == 5:
+                if k == 7:
                     nc.sync.dma_start(out=z1t[:], in_=rows(z1))
 
                 for j in range(J):
@@ -436,26 +449,25 @@ def tile_cn_pa_v_kernel(tc, x, cond, W1, b1, W2, b2, z1, p, num, den, grad_out, 
 
             for task in pend:
                 task()
+            s_out(NU - 1)
+            tail = [turn_dp(J - 1, pair, "vector" if i % 2 else "scalar") for i, pair in enumerate(pairs[NU - 1])]
+            for task in tail:
+                task()
             for j, s in mx_ready:
                 mx(j, s)
             for j in range(J):
-                if j not in stage:
+                at = stage[j][1] if j in stage else "none"
+                if at == "none":
                     dz_mask(j)
+                if at in ("none", "mask"):
                     dz_turn(j)()
+                if at in ("none", "mask", "turn"):
                     dz_mx(j)
-                    dz_store(j)
-                elif stage[j][1] == "mask":
-                    dz_turn(j)()
-                    dz_mx(j)
-                    dz_store(j)
-                elif stage[j][1] == "turn":
-                    dz_mx(j)
-                    dz_store(j)
-                elif stage[j][1] == "mx":
+                if at != "store":
                     dz_store(j)
             nc.vector.tensor_copy(dzi[:], dz[:].rearrange("p j h -> p h j"))
             nc.vector.quantize_mx(out=dziq[:].bitcast(E5M2), scales=dzis[:], in_=dzi[:].rearrange("p h j -> p (h j)"))
-            o1 = psum.tile([P, HID], F32, name="acc", bufs=3)
+            o1 = psum.tile([P, HID], F32, name="acc", bufs=2)
             nc.tensor.matmul_mx(out=o1[:], lhsT=cdq[:].bitcast(E4M3), lhsT_scale=cds[:], rhs=dziq[:].bitcast(E5M2), rhs_scale=dzis[:], start=True, stop=True)
             ob1 = work.tile([P, HID], F32, name="ob1", bufs=1)
             nc.scalar.copy(ob1[:], o1[:])

@@ -21,19 +21,17 @@ PASS = 512
 PASSES = NCOL // PASS
 PC = 9216
 
-SIZES = [[8, 24, 32, 32, 32], [32, 32, 32, 32], [32, 32, 32, 32], [32, 32, 32, 24, 8]]
+SIZES = [[8, 16, 22, 22, 20, 20, 20], [22, 22, 22, 22, 20, 20], [22, 22, 22, 22, 20, 20], [22, 22, 22, 22, 20, 12, 8]]
 CW = max(max(s) for s in SIZES) * LS
 UNITS = [(j, sum(SIZES[j][:c]), n) for j in range(J) for c, n in enumerate(SIZES[j])]
 NU = len(UNITS)
-W2_STEPS = 10
-ADD_ON_TENSOR = range(4, 14)
-T1_ON_SCALAR = 3
+W2_STEPS = 14
 
 FLOPS = 2 * B * NCOL * HID + 2 * 2 * B * HID * DIM
 BYTES = B * (PC - DIM) * 4 + HID * PC * 2 + 3 * B * DIM * 2 + DIM * HID * 2 + B * HID * 4 + 2 * B * DIM * 4 + 2 * B * DIM * 4
 
 
-def pairs_by_unit():
+def groups_by_unit():
     result = []
     for j in range(J):
         ends = [sum(SIZES[j][: c + 1]) * LS for c in range(len(SIZES[j]))]
@@ -42,23 +40,28 @@ def pairs_by_unit():
             return min(c for c in range(len(ends)) if k % SEC < ends[c]) if k < 3 * SEC else 0
 
         ready = [max(chunk(k) for k in range(PASS * g, PASS * (g + 1))) for g in range(PASSES)]
-        order = sorted(range(PASSES), key=lambda g: (ready[g], g))
-        pairs = [[] for c in ends]
-        for s in range(PASSES // 2):
-            a, b = order[2 * s], order[2 * s + 1]
-            pairs[max(ready[a], ready[b])].append((s, a, b))
-        result.extend(pairs)
+        size = 4 if j < J - 1 else 2
+        waiting = []
+        slot = 0
+        for c in range(len(ends)):
+            groups = []
+            waiting += [g for g in range(PASSES) if ready[g] == c]
+            while len(waiting) >= size or (waiting and c == len(ends) - 1):
+                groups.append((slot, waiting[:size]))
+                slot += len(waiting[:size])
+                waiting = waiting[size:]
+            result.append(groups)
     return result
 
 
 def tile_cn_pa_v_kernel(tc, x, cond, W1, b1, W2, b2, z1, p, num, den, grad_out, out_0, out_1):
     nc = tc.nc
-    pairs = pairs_by_unit()
+    groups = groups_by_unit()
     slot_pass = {}
     for i, (j, d0, n) in enumerate(UNITS):
-        for s, a, b in pairs[i]:
-            slot_pass[j, 2 * s] = a
-            slot_pass[j, 2 * s + 1] = b
+        for slot, passes in groups[i]:
+            for s, g in enumerate(passes):
+                slot_pass[j, slot + s] = g
     w2_at = {k: range(k * PASSES // W2_STEPS, (k + 1) * PASSES // W2_STEPS) for k in range(W2_STEPS)}
 
     def rows(ap):
@@ -81,7 +84,6 @@ def tile_cn_pa_v_kernel(tc, x, cond, W1, b1, W2, b2, z1, p, num, den, grad_out, 
         rr = keep.tile([P, J, DIM], F32, name="rr")
         dn = keep.tile([P, J, DIM], F32, name="dn")
         ea = keep.tile([P, J, 2 * DIM], F32, name="ea")
-        xf = keep.tile([P, J, DIM], F32, name="xf")
         sg = keep.tile([P, J, DIM], F32, name="sg")
         om = keep.tile([P, J, DIM], F32, name="om")
         tt = keep.tile([P, J, DIM], F32, name="tt")
@@ -105,27 +107,30 @@ def tile_cn_pa_v_kernel(tc, x, cond, W1, b1, W2, b2, z1, p, num, den, grad_out, 
         with tc.manual_schedule():
             tiles = {}
 
-            def load_unit(i):
+            def load(name, i):
+                if (name, i) in tiles or not 0 <= i < NU:
+                    return
+                sec, bufs = {"A": (0, 5), "B": (1, 3), "C": (2, 5)}[name]
                 j, d0, n = UNITS[i]
-                for name, sec, bufs in (("A", 0, 3), ("C", 2, 4), ("B", 1, 4)):
-                    t = work.tile([P, CW], F32, name="pin" + name, bufs=bufs)
-                    nc.sync.dma_start(out=t[:, : n * LS], in_=rows(p)[:, j, sec * SEC + d0 * LS : sec * SEC + (d0 + n) * LS])
-                    tiles[name, i] = t[:, : n * LS]
+                t = work.tile([P, CW], F32, name="in" + name, bufs=bufs)[:, : n * LS]
+                nc.sync.dma_start(out=t, in_=rows(p)[:, j, sec * SEC + d0 * LS : sec * SEC + (d0 + n) * LS])
+                tiles[name, i] = t
 
             def load_w2(g):
-                t = work.tile([P, HID // P, PASS], BF16, name="w2r", bufs=2, align_bytes=64)
+                t = work.tile([P, HID // P, PASS], BF16, name="w2r", bufs=3, align_bytes=64)
                 nc.sync.dma_start(out=t[:], in_=W2.rearrange("(h q) k -> q h k", q=P)[:, :, PASS * g : PASS * (g + 1)])
                 tiles["w2r", g] = t
 
             nc.sync.dma_start(out=xb[:], in_=rows(x))
-            load_unit(0)
+            load("A", 0)
+            load("B", 0)
             nc.sync.dma_start(out=dn[:], in_=rows(den))
             nc.sync.dma_start(out=rr[:], in_=rows(num))
             nc.sync.dma_start(out=ea[:], in_=rows(p)[:, :, PC - 2 * DIM :])
+            load("C", 0)
             nc.sync.dma_start(out=gb[:], in_=rows(grad_out))
-            load_unit(1)
-            for g in w2_at[0]:
-                load_w2(g)
+            for name in "ABC":
+                load(name, 1)
 
             def small_a(a, b):
                 v = nc.vector
@@ -145,9 +150,8 @@ def tile_cn_pa_v_kernel(tc, x, cond, W1, b1, W2, b2, z1, p, num, den, grad_out, 
                 v.scalar_tensor_tensor(last[:, a:b, 2 * DIM :], tt[:, a:b], 0.1, c0, ALU.mult, ALU.mult)
                 v.tensor_tensor(last[:, a:b, DIM : 2 * DIM], c1, om[:, a:b], ALU.mult)
 
-            def bc(t, i, n=None):
-                j, d0, size = UNITS[i]
-                n = size if n is None else n
+            def bc(t, i):
+                j, d0, n = UNITS[i]
                 return t[:, j, d0 : d0 + n].unsqueeze(2).to_broadcast([P, n, LS])
 
             def v3(t):
@@ -157,12 +161,42 @@ def tile_cn_pa_v_kernel(tc, x, cond, W1, b1, W2, b2, z1, p, num, den, grad_out, 
                 tiles[key, i] = work.tile([P, CW], F32, name="t" + key, bufs=bufs)[:, : UNITS[i][2] * LS]
                 return tiles[key, i]
 
-            def s_m(i):
-                j, d0, n = UNITS[i]
-                m = new_tile("E", i, 3)
-                for d in range(n):
-                    run = slice(d * LS, (d + 1) * LS)
-                    nc.scalar.activation(m[:, run], tiles["A", i][:, run], ACT.Copy, scale=xf[:, j, d0 + d : d0 + d + 1])
+            def blocks(i):
+                w = UNITS[i][2] * LS
+                return [min(P * b, w - P) for b in range((w + P - 1) // P)]
+
+            def g_m(i):
+                nc.gpsimd.tensor_tensor(v3(new_tile("M", i, 3)), v3(tiles["A", i]), bc(xb, i), ALU.mult)
+
+            def g_w(i):
+                nc.gpsimd.tensor_tensor(new_tile("W", i, 2), tiles["A", i], tiles["C", i], ALU.mult)
+
+            def pe_z(i):
+                zt = psum.tile([P, 4, P], F32, name="zt", bufs=1)
+                tiles["ZT", i] = zt
+                for b, c in enumerate(blocks(i)):
+                    nc.tensor.matmul(zt[:, b, :], lhsT=tiles["M", i][:, c : c + P], rhs=ident[:], is_transpose=True, start=True, stop=False)
+                    nc.tensor.matmul(zt[:, b, :], lhsT=tiles["B", i][:, c : c + P], rhs=ident[:], is_transpose=True, start=False, stop=True)
+
+            def s_exp(i):
+                nb = len(blocks(i))
+                et = work.tile([P, 4, P], F32, name="et", bufs=2)
+                tiles["ET", i] = et
+                nc.scalar.activation(et[:, :nb, :], tiles["ZT", i][:, :nb, :], ACT.Relu, scale=-1.0)
+                nc.scalar.activation(et[:, :nb, :], et[:, :nb, :], ACT.Exp, scale=-1.0)
+
+            def v_s1(i):
+                nb = len(blocks(i))
+                st = work.tile([P, 4, P], F32, name="st", bufs=2)
+                tiles["ST", i] = st
+                nc.vector.scalar_tensor_tensor(st[:, :nb, :], tiles["ZT", i][:, :nb, :], 0.0, tiles["ET", i][:, :nb, :], ALU.max, ALU.add)
+
+            def pe_back(i):
+                for src, dst in (("ST", "SB"), ("ET", "EB")):
+                    bank = psum.tile([P, HID], F32, name="b" + dst, bufs=1)
+                    tiles[dst, i] = bank[:, : UNITS[i][2] * LS]
+                    for b, c in enumerate(blocks(i)):
+                        nc.tensor.transpose(bank[:, c : c + P], tiles[src, i][:, b, :], ident[:])
 
             def s_out(i):
                 j, d0, n = UNITS[i]
@@ -175,19 +209,8 @@ def tile_cn_pa_v_kernel(tc, x, cond, W1, b1, W2, b2, z1, p, num, den, grad_out, 
                         scale=dd[:, j, d0 + d : d0 + d + 1],
                     )
 
-            def s_exp(i):
-                e = tiles["E", i]
-                nc.scalar.activation(e, tiles["B", i], ACT.Relu, scale=-1.0)
-                nc.scalar.activation(e, e, ACT.Exp, scale=-1.0)
-
             def y(i, s):
                 return tiles["Y", i][:, s, : UNITS[i][2] * LS]
-
-            def v_z(i):
-                nc.vector.tensor_tensor(tiles["B", i], tiles["E", i], tiles["B", i], ALU.add)
-
-            def v_w(i):
-                nc.vector.tensor_tensor(new_tile("W", i, 2), tiles["A", i], tiles["C", i], ALU.mult)
 
             def v_q(i):
                 w = v3(tiles["W", i])
@@ -196,49 +219,22 @@ def tile_cn_pa_v_kernel(tc, x, cond, W1, b1, W2, b2, z1, p, num, den, grad_out, 
             def v_qa(i):
                 nc.vector.tensor_tensor(new_tile("QA", i, 2), tiles["W", i], tiles["A", i], ALU.mult)
 
-            def t1_scalar(i):
-                return UNITS[i][2] * T1_ON_SCALAR // 8
-
-            def s_t1(i):
-                yt = work.tile([P, 3, CW], F32, name="yt", bufs=2)
-                tiles["Y", i] = yt
-                j, d0, n = UNITS[i]
-                for d in range(n - t1_scalar(i), n):
-                    run = slice(d * LS, (d + 1) * LS)
-                    nc.scalar.activation(y(i, 0)[:, run], tiles["E", i][:, run], ACT.Copy, scale=xf[:, j, d0 + d : d0 + d + 1])
-
             def v_t1(i):
-                n = UNITS[i][2] - t1_scalar(i)
-                nc.vector.tensor_tensor(v3(y(i, 0)[:, : n * LS]), v3(tiles["E", i][:, : n * LS]), bc(xf, i, n), ALU.mult)
-
-            def pe_t2(i):
-                half = UNITS[i][2] * LS // 2
-                tiles["t2", i] = psum.tile([P, 2, HID], F32, name="t2", bufs=1)
-                for h in range(2):
-                    cols = slice(h * half, (h + 1) * half)
-                    out = tiles["t2", i][:, h, :half]
-                    nc.tensor.matmul(out, lhsT=ident[:], rhs=y(i, 0)[:, cols], start=True, stop=False)
-                    nc.tensor.matmul(out, lhsT=ident[:], rhs=tiles["W", i][:, cols], start=False, stop=True)
+                yt = work.tile([P, 3, CW], F32, name="yt", bufs=3)
+                tiles["Y", i] = yt
+                nc.vector.tensor_tensor(v3(y(i, 0)), v3(tiles["EB", i]), bc(xb, i), ALU.mult)
 
             def v_t2(i):
                 nc.vector.tensor_tensor(y(i, 0), y(i, 0), tiles["W", i], ALU.add)
-
-            def v_y1_psum(i, h):
-                half = UNITS[i][2] * LS // 2
-                cols = slice(h * half, (h + 1) * half)
-                nc.vector.tensor_tensor(y(i, 0)[:, cols], tiles["t2", i][:, h, :half], tiles["C", i][:, cols], ALU.mult)
 
             def v_y1(i):
                 nc.vector.tensor_tensor(y(i, 0), y(i, 0), tiles["C", i], ALU.mult)
 
             def v_y2(i):
-                nc.vector.tensor_tensor(y(i, 1), tiles["E", i], tiles["C", i], ALU.mult)
-
-            def v_s1(i):
-                nc.vector.scalar_tensor_tensor(y(i, 2), tiles["B", i], 0.0, tiles["E", i], ALU.max, ALU.add)
+                nc.vector.tensor_tensor(y(i, 1), tiles["EB", i], tiles["C", i], ALU.mult)
 
             def v_s2(i):
-                nc.vector.scalar_tensor_tensor(y(i, 2), tiles["QA", i], -1.0, y(i, 2), ALU.add, ALU.add)
+                nc.vector.scalar_tensor_tensor(y(i, 2), tiles["SB", i], -1.0, tiles["QA", i], ALU.add, ALU.add)
 
             def v_last(j):
                 nc.vector.tensor_copy(dp[:, 3 * SEC :], last[:, j, :])
@@ -249,24 +245,26 @@ def tile_cn_pa_v_kernel(tc, x, cond, W1, b1, W2, b2, z1, p, num, den, grad_out, 
                 else:
                     nc.scalar.copy(out, bank)
 
-            def turn_dp(j, pair, engine="scalar"):
-                s, a, b = pair
+            def turn_dp(j, group, engine="scalar"):
+                slot, passes = group
+                size = len(passes)
                 words = dp[:].bitcast(F32)
-                bank = psum.tile([P, 2, 2, P], F32, name="tr", bufs=4)
-                for h, g in enumerate((a, b)):
-                    for u in range(2):
-                        nc.tensor.transpose(bank[:, h, u, :], words[:, 256 * g + u : 256 * (g + 1) : 2], ident[:])
-                grp = work.tile([P, 2 * P * 4], BF16, name="dpg", bufs=4, align_bytes=64)
-                copy_words(engine, grp[:].bitcast(F32).rearrange("p (h r u) -> p h r u", h=2, u=2), bank[:].rearrange("p h u r -> p h r u"))
+                grp = work.tile([P, 4 * P * 4], BF16, name="dpg", bufs=3, align_bytes=64)
+                for half in range(0, size, 2):
+                    bank = psum.tile([P, 2, 2, P], F32, name="tr", bufs=3)
+                    for h, g in enumerate(passes[half : half + 2]):
+                        for u in range(2):
+                            nc.tensor.transpose(bank[:, h, u, :], words[:, 256 * g + u : 256 * (g + 1) : 2], ident[:])
+                    out = grp[:].bitcast(F32)[:, half * 256 : half * 256 + 512].rearrange("p (h r u) -> p h r u", h=2, u=2)
+                    copy_words(engine, out, bank[:].rearrange("p h u r -> p h r u"))
 
                 def quant():
                     if ("dpq", j) not in tiles:
                         tiles["dpq", j] = work.tile([P, PASSES * P], U32, name="dpq", bufs=2, align_bytes=64)
                         tiles["dps", j] = work.tile([P, PASSES * P], U8, name="dps", bufs=2, align_bytes=64)
-                    cols = slice(2 * s * P, (2 * s + 2) * P)
-                    nc.vector.quantize_mx(out=tiles["dpq", j][:, cols].bitcast(E5M2), scales=tiles["dps", j][:, cols], in_=grp[:])
-                    mx_ready.append((j, 2 * s))
-                    mx_ready.append((j, 2 * s + 1))
+                    cols = slice(slot * P, (slot + size) * P)
+                    nc.vector.quantize_mx(out=tiles["dpq", j][:, cols].bitcast(E5M2), scales=tiles["dps", j][:, cols], in_=grp[:, : size * P * 4])
+                    mx_ready.extend((j, slot + s) for s in range(size))
 
                 return quant
 
@@ -274,7 +272,7 @@ def tile_cn_pa_v_kernel(tc, x, cond, W1, b1, W2, b2, z1, p, num, den, grad_out, 
                 words = tiles["w2r", g][:].bitcast(F32)
                 grp = work.tile([P, HID * 4], BF16, name="w2g", bufs=2, align_bytes=64)
                 for half in range(2):
-                    bank = psum.tile([P, 2, 2, P], F32, name="tr", bufs=4)
+                    bank = psum.tile([P, 2, 2, P], F32, name="tr", bufs=3)
                     for h in range(2):
                         for u in range(2):
                             nc.tensor.transpose(bank[:, h, u, :], words[:, 2 * half + h, u:256:2], ident[:])
@@ -313,7 +311,7 @@ def tile_cn_pa_v_kernel(tc, x, cond, W1, b1, W2, b2, z1, p, num, den, grad_out, 
 
             def dz_turn(j):
                 words = dz[:, j, :].bitcast(F32)
-                bank = psum.tile([P, 2, P], F32, name="tr", bufs=4)
+                bank = psum.tile([P, 2, P], F32, name="tr", bufs=3)
                 for u in range(2):
                     nc.tensor.transpose(bank[:, u, :], words[:, u:256:2], ident[:])
                 grp = work.tile([P, P * 4], BF16, name="dzg", bufs=2, align_bytes=64)
@@ -340,7 +338,7 @@ def tile_cn_pa_v_kernel(tc, x, cond, W1, b1, W2, b2, z1, p, num, den, grad_out, 
 
             def w1_turn():
                 words = w1r[:].bitcast(F32)
-                bank = psum.tile([P, 2, P], F32, name="tr", bufs=4)
+                bank = psum.tile([P, 2, P], F32, name="tr", bufs=3)
                 for u in range(2):
                     nc.tensor.transpose(bank[:, u, :], words[:, u:256:2], ident[:])
                 nc.scalar.copy(w1g[:].bitcast(F32).rearrange("p (r u) -> p r u", u=2), bank[:].rearrange("p u r -> p r u"))
@@ -356,41 +354,41 @@ def tile_cn_pa_v_kernel(tc, x, cond, W1, b1, W2, b2, z1, p, num, den, grad_out, 
 
             nc.vector.memset(sg[:, 0, 0:1], 0.0)
             nc.scalar.activation(sg[:, 0, 0:1], sg[:, 0, 0:1], ACT.Sigmoid)
-            nc.vector.tensor_copy(xf[:], xb[:])
-            s_m(0)
             nc.scalar.activation(sg[:], ea[:, :, 0:DIM], ACT.Sigmoid, scale=0.1)
             nc.scalar.activation(om[:], ea[:, :, 0:DIM], ACT.Sigmoid, scale=-0.1)
             nc.scalar.activation(tt[:], ea[:, :, DIM:], ACT.Exp, scale=0.1)
 
+            def has(i):
+                return 0 <= i < NU
+
             pend = []
             stage = {}
-            for k in range(-1, NU):
+            for k in range(-3, NU + 2):
                 new = []
-                nxt = k + 1 < NU
-                cur = k >= 0
-                if cur:
-                    s_t1(k)
-                if k >= 1:
-                    s_out(k - 1)
-                if nxt:
-                    v_z(k + 1)
-                    s_exp(k + 1)
-                if cur:
+                if has(k + 1):
+                    g_w(k + 1)
+                if has(k + 3):
+                    g_m(k + 3)
+                if has(k - 2):
+                    s_out(k - 2)
+                if has(k):
                     v_t1(k)
-                if k in ADD_ON_TENSOR:
-                    pe_t2(k)
-                if k >= 1:
-                    for pair in pairs[k - 1]:
-                        new.append(turn_dp(UNITS[k - 1][0], pair))
-                if k + 2 < NU:
-                    s_m(k + 2)
+                    v_y2(k)
+                    v_s2(k)
+                if has(k + 1):
+                    v_s1(k + 1)
+                    pe_back(k + 1)
+                if has(k + 2):
+                    pe_z(k + 2)
+                    s_exp(k + 2)
+                if has(k - 2):
+                    for n, group in enumerate(groups[k - 2]):
+                        new.append(turn_dp(UNITS[k - 2][0], group, "vector" if k == NU + 1 and n % 2 else "scalar"))
                 for g in w2_at.get(k, []):
                     new.append(turn_w2(g))
                 if k == 2:
                     w1_turn()
-                    new.append(w1_quant)
-                    new.append(cond_group)
-                    new.append(cond_quant)
+                    new += [w1_quant, cond_group, cond_quant]
                 for j in range(J):
                     if stage.get(j) == (k - 1, "mask"):
                         new.append(dz_turn(j))
@@ -399,40 +397,42 @@ def tile_cn_pa_v_kernel(tc, x, cond, W1, b1, W2, b2, z1, p, num, den, grad_out, 
                         dz_store(j)
                         stage[j] = (k, "store")
 
-                todo = []
-                if k == -1:
-                    todo += [lambda: v_w(0), lambda: small_a(0, J), lambda: v_q(0), lambda: v_qa(0), lambda: small_b(0, J)]
-                else:
-                    second = [lambda: v_w(k + 1), lambda: v_q(k + 1), lambda: v_qa(k + 1)] if nxt else []
-                    if k in ADD_ON_TENSOR:
-                        todo += second[:1] + [lambda: v_s1(k)] + second[1:2] + [lambda: v_y2(k), lambda: v_s2(k)] + second[2:]
-                        todo += [lambda: v_y1_psum(k, 0), lambda: v_y1_psum(k, 1)]
-                    else:
-                        todo += second[:1] + [lambda: v_t2(k)] + second[1:2] + [lambda: v_s1(k), lambda: v_y1(k)] + second[2:]
-                        todo += [lambda: v_s2(k), lambda: v_y2(k)]
-                if cur and UNITS[k][1] == SIZES[UNITS[k][0]][0]:
-                    todo.append(lambda: v_last(UNITS[k][0]))
-                w2_was = len(w2_done)
                 ready_now = len(mx_ready)
-                n = max(len(todo), 1)
+                todo = []
+                if k == -2:
+                    todo.append(lambda: small_a(0, J))
+                if has(k + 1):
+                    todo.append(lambda: v_q(k + 1))
+                if has(k - 1):
+                    todo.append(lambda: v_y1(k - 1))
+                if has(k + 1):
+                    todo.append(lambda: v_qa(k + 1))
+                if k == -1:
+                    todo.append(lambda: small_b(0, J))
+                if has(k) and UNITS[k][1] == SIZES[UNITS[k][0]][0]:
+                    todo.append(lambda: v_last(UNITS[k][0]))
+                slots = len(todo)
                 done = 0
-                for m in range(n):
-                    if m < len(todo):
-                        todo[m]()
-                    want = len(pend) * (m + 1) // n
-                    while done < want:
+                for m in range(slots):
+                    todo[m]()
+                    while done < len(pend) * (m + 1) // slots:
                         pend[done]()
                         done += 1
+                for task in pend[done:]:
+                    task()
+                if has(k):
+                    v_t2(k)
                 pend = new
 
-                if k + 3 < NU:
-                    load_unit(k + 3)
-                for g in w2_at.get(k + 1, []) if k >= 0 else []:
+                load("A", k + 5)
+                load("B", k + 4)
+                load("C", k + 3)
+                for g in w2_at.get(k + 1, []):
                     load_w2(g)
                 if k == 0:
                     nc.sync.dma_start(out=w1r[:], in_=W1)
                     nc.sync.dma_start(out=cdr[:], in_=rows(cond))
-                if k == 7:
+                if k == 10:
                     nc.sync.dma_start(out=z1t[:], in_=rows(z1))
 
                 for j in range(J):
@@ -448,10 +448,6 @@ def tile_cn_pa_v_kernel(tc, x, cond, W1, b1, W2, b2, z1, p, num, den, grad_out, 
                     mx_ready = mx_ready[take:]
 
             for task in pend:
-                task()
-            s_out(NU - 1)
-            tail = [turn_dp(J - 1, pair, "vector" if i % 2 else "scalar") for i, pair in enumerate(pairs[NU - 1])]
-            for task in tail:
                 task()
             for j, s in mx_ready:
                 mx(j, s)

@@ -25,7 +25,8 @@ SIZES = [[8, 16, 22, 22, 20, 20, 20], [22, 22, 22, 22, 20, 20], [22, 22, 22, 22,
 CW = max(max(s) for s in SIZES) * LS
 UNITS = [(j, sum(SIZES[j][:c]), n) for j in range(J) for c, n in enumerate(SIZES[j])]
 NU = len(UNITS)
-W2_STEPS = 14
+W2_STEPS = 16
+MX_A_STEP = 9
 
 FLOPS = 2 * B * NCOL * HID + 2 * 2 * B * HID * DIM
 BYTES = B * (PC - DIM) * 4 + HID * PC * 2 + 3 * B * DIM * 2 + DIM * HID * 2 + B * HID * 4 + 2 * B * DIM * 4 + 2 * B * DIM * 4
@@ -62,7 +63,8 @@ def tile_cn_pa_v_kernel(tc, x, cond, W1, b1, W2, b2, z1, p, num, den, grad_out, 
         for slot, passes in groups[i]:
             for s, g in enumerate(passes):
                 slot_pass[j, slot + s] = g
-    w2_at = {k: range(k * PASSES // W2_STEPS, (k + 1) * PASSES // W2_STEPS) for k in range(W2_STEPS)}
+    w2_order = [slot_pass[0, s] for s in range(PASSES)]
+    w2_at = {k: w2_order[k * PASSES // W2_STEPS : (k + 1) * PASSES // W2_STEPS] for k in range(W2_STEPS)}
 
     def rows(ap):
         return ap.rearrange("(p j) w -> p j w", j=J)
@@ -83,7 +85,8 @@ def tile_cn_pa_v_kernel(tc, x, cond, W1, b1, W2, b2, z1, p, num, den, grad_out, 
         gb = keep.tile([P, J, DIM], BF16, name="gb")
         rr = keep.tile([P, J, DIM], F32, name="rr")
         dn = keep.tile([P, J, DIM], F32, name="dn")
-        ea = keep.tile([P, J, 2 * DIM], F32, name="ea")
+        ea = keep.tile([P, J, 2 * DIM], F32, name="ea", align_bytes=64)
+        xf = keep.tile([P, J, DIM], F32, name="xf")
         sg = keep.tile([P, J, DIM], F32, name="sg")
         om = keep.tile([P, J, DIM], F32, name="om")
         tt = keep.tile([P, J, DIM], F32, name="tt")
@@ -92,7 +95,6 @@ def tile_cn_pa_v_kernel(tc, x, cond, W1, b1, W2, b2, z1, p, num, den, grad_out, 
         dp = keep.tile([P, NCOL], BF16, name="dp", align_bytes=64)
         w2q = keep.tile([P, PASSES, HID], U32, name="w2q", align_bytes=64)
         w2s = keep.tile([P, PASSES, HID], U8, name="w2s", align_bytes=64)
-        z1t = keep.tile([P, J, HID], F32, name="z1t")
         dz = keep.tile([P, J, HID], BF16, name="dz", align_bytes=64)
         w1r = keep.tile([P, HID], BF16, name="w1r", align_bytes=64)
         w1g = keep.tile([P, HID], BF16, name="w1g", align_bytes=64)
@@ -100,7 +102,6 @@ def tile_cn_pa_v_kernel(tc, x, cond, W1, b1, W2, b2, z1, p, num, den, grad_out, 
         cdg = keep.tile([P, DIM, J], BF16, name="cdg", align_bytes=64)
         cdq = keep.tile([P, DIM], U32, name="cdq", align_bytes=64)
         cds = keep.tile([P, DIM], U8, name="cds", align_bytes=64)
-        dzi = keep.tile([P, HID, J], BF16, name="dzi", align_bytes=64)
         dziq = keep.tile([P, HID], U32, name="dziq", align_bytes=64)
         dzis = keep.tile([P, HID], U8, name="dzis", align_bytes=64)
 
@@ -121,24 +122,31 @@ def tile_cn_pa_v_kernel(tc, x, cond, W1, b1, W2, b2, z1, p, num, den, grad_out, 
                 nc.sync.dma_start(out=t[:], in_=W2.rearrange("(h q) k -> q h k", q=P)[:, :, PASS * g : PASS * (g + 1)])
                 tiles["w2r", g] = t
 
+            pairs_in = ((dn, rows(den)), (rr, rows(num)), (ea, rows(p)[:, :, PC - 2 * DIM :]), (gb, rows(grad_out)))
             nc.sync.dma_start(out=xb[:], in_=rows(x))
             load("A", 0)
-            load("B", 0)
-            nc.sync.dma_start(out=dn[:], in_=rows(den))
-            nc.sync.dma_start(out=rr[:], in_=rows(num))
-            nc.sync.dma_start(out=ea[:], in_=rows(p)[:, :, PC - 2 * DIM :])
             load("C", 0)
-            nc.sync.dma_start(out=gb[:], in_=rows(grad_out))
-            for name in "ABC":
-                load(name, 1)
+            load("B", 0)
+            for t, src in pairs_in[:2]:
+                nc.sync.dma_start(out=t[:, 0:1], in_=src[:, 0:1])
+            load("A", 1)
+            load("C", 1)
+            load("B", 1)
+            load("A", 2)
+            for t, src in pairs_in[2:]:
+                nc.sync.dma_start(out=t[:], in_=src)
+            load("B", 2)
+            for t, src in pairs_in[:2]:
+                nc.sync.dma_start(out=t[:, 1:], in_=src[:, 1:])
 
-            def small_a(a, b):
-                v = nc.vector
-                v.reciprocal(dn[:, a:b], dn[:, a:b])
-                v.tensor_tensor(tt[:, a:b], gb[:, a:b], tt[:, a:b], ALU.mult)
-                v.tensor_tensor(rr[:, a:b], rr[:, a:b], dn[:, a:b], ALU.mult)
-                v.tensor_tensor(dn[:, a:b], sg[:, a:b], dn[:, a:b], ALU.mult)
-                v.scalar_tensor_tensor(dd[:, a:b], tt[:, a:b], 0.8, dn[:, a:b], ALU.mult, ALU.mult)
+            def small_r(a, b):
+                nc.vector.reciprocal(dn[:, a:b], dn[:, a:b])
+                nc.vector.tensor_tensor(rr[:, a:b], rr[:, a:b], dn[:, a:b], ALU.mult)
+
+            def small_d(a, b):
+                nc.vector.tensor_tensor(tt[:, a:b], gb[:, a:b], tt[:, a:b], ALU.mult)
+                nc.vector.tensor_tensor(dn[:, a:b], sg[:, a:b], dn[:, a:b], ALU.mult)
+                nc.vector.scalar_tensor_tensor(dd[:, a:b], tt[:, a:b], 0.8, dn[:, a:b], ALU.mult, ALU.mult)
 
             def small_b(a, b):
                 v = nc.vector
@@ -150,9 +158,17 @@ def tile_cn_pa_v_kernel(tc, x, cond, W1, b1, W2, b2, z1, p, num, den, grad_out, 
                 v.scalar_tensor_tensor(last[:, a:b, 2 * DIM :], tt[:, a:b], 0.1, c0, ALU.mult, ALU.mult)
                 v.tensor_tensor(last[:, a:b, DIM : 2 * DIM], c1, om[:, a:b], ALU.mult)
 
-            def bc(t, i):
-                j, d0, n = UNITS[i]
+            def bc(t, i, n=None):
+                j, d0, size = UNITS[i]
+                n = size if n is None else n
                 return t[:, j, d0 : d0 + n].unsqueeze(2).to_broadcast([P, n, LS])
+
+            def v_out(i):
+                j, d0, n = UNITS[i]
+                out = dp[:, : 3 * SEC].rearrange("p (s w) -> p s w", s=3)[:, :, d0 * LS : (d0 + n) * LS].rearrange("p s (d l) -> p s d l", l=LS)
+                src = tiles["Y", i][:, :, : n * LS].rearrange("p s (d l) -> p s d l", l=LS)
+                for s in range(2):
+                    nc.vector.tensor_tensor(out[:, s], src[:, s], bc(dd, i), ALU.mult)
 
             def v3(t):
                 return t.rearrange("p (d l) -> p d l", l=LS)
@@ -165,11 +181,16 @@ def tile_cn_pa_v_kernel(tc, x, cond, W1, b1, W2, b2, z1, p, num, den, grad_out, 
                 w = UNITS[i][2] * LS
                 return [min(P * b, w - P) for b in range((w + P - 1) // P)]
 
-            def g_m(i):
-                nc.gpsimd.tensor_tensor(v3(new_tile("M", i, 3)), v3(tiles["A", i]), bc(xb, i), ALU.mult)
+            def make_m(i):
+                j, d0, n = UNITS[i]
+                m, a = new_tile("M", i, 3), tiles["A", i]
+                for d in range(n):
+                    run = slice(d * LS, (d + 1) * LS)
+                    nc.scalar.activation(m[:, run], a[:, run], ACT.Copy, scale=xf[:, j, d0 + d : d0 + d + 1])
 
-            def g_w(i):
-                nc.gpsimd.tensor_tensor(new_tile("W", i, 2), tiles["A", i], tiles["C", i], ALU.mult)
+            def make_w(i):
+                engine = nc.vector if i < 2 else nc.gpsimd
+                engine.tensor_tensor(new_tile("W", i, 2), tiles["A", i], tiles["C", i], ALU.mult)
 
             def pe_z(i):
                 zt = psum.tile([P, 4, P], F32, name="zt", bufs=1)
@@ -187,23 +208,29 @@ def tile_cn_pa_v_kernel(tc, x, cond, W1, b1, W2, b2, z1, p, num, den, grad_out, 
 
             def v_s1(i):
                 nb = len(blocks(i))
-                st = work.tile([P, 4, P], F32, name="st", bufs=2)
+                st = work.tile([P, 4, P], F32, name="st", bufs=3)
                 tiles["ST", i] = st
                 nc.vector.scalar_tensor_tensor(st[:, :nb, :], tiles["ZT", i][:, :nb, :], 0.0, tiles["ET", i][:, :nb, :], ALU.max, ALU.add)
 
             def pe_back(i):
-                for src, dst in (("ST", "SB"), ("ET", "EB")):
-                    bank = psum.tile([P, HID], F32, name="b" + dst, bufs=1)
-                    tiles[dst, i] = bank[:, : UNITS[i][2] * LS]
-                    for b, c in enumerate(blocks(i)):
-                        nc.tensor.transpose(bank[:, c : c + P], tiles[src, i][:, b, :], ident[:])
+                bank = psum.tile([P, HID], F32, name="eb", bufs=1)
+                tiles["EB", i] = bank[:, : UNITS[i][2] * LS]
+                for b, c in enumerate(blocks(i)):
+                    nc.tensor.transpose(bank[:, c : c + P], tiles["ET", i][:, b, :], ident[:])
+
+            def pe_sum(i):
+                bank = psum.tile([P, HID], F32, name="sb", bufs=1)
+                tiles["SB", i] = bank[:, : UNITS[i][2] * LS]
+                for b, c in enumerate(blocks(i)):
+                    nc.tensor.matmul(bank[:, c : c + P], lhsT=tiles["ST", i][:, b, :], rhs=ident[:], is_transpose=True, start=True, stop=False)
+                    nc.tensor.matmul(bank[:, c : c + P], lhsT=ident[:], rhs=tiles["QA", i][:, c : c + P], start=False, stop=True)
 
             def s_out(i):
                 j, d0, n = UNITS[i]
                 out = dp[:, : 3 * SEC].rearrange("p (s w) -> p s w", s=3)
                 for d in range(n):
                     nc.scalar.activation(
-                        out[:, :, (d0 + d) * LS : (d0 + d + 1) * LS],
+                        out[:, 0:2, (d0 + d) * LS : (d0 + d + 1) * LS],
                         tiles["Y", i][:, :, d * LS : (d + 1) * LS],
                         ACT.Copy,
                         scale=dd[:, j, d0 + d : d0 + d + 1],
@@ -216,11 +243,12 @@ def tile_cn_pa_v_kernel(tc, x, cond, W1, b1, W2, b2, z1, p, num, den, grad_out, 
                 w = v3(tiles["W", i])
                 nc.vector.scalar_tensor_tensor(w, w, 0.0, bc(rr, i), ALU.is_lt, ALU.mult)
 
-            def v_qa(i):
-                nc.vector.tensor_tensor(new_tile("QA", i, 2), tiles["W", i], tiles["A", i], ALU.mult)
+            def make_qa(i):
+                engine = nc.vector if i < 1 else nc.gpsimd
+                engine.tensor_tensor(new_tile("QA", i, 2), tiles["W", i], tiles["A", i], ALU.mult)
 
             def v_t1(i):
-                yt = work.tile([P, 3, CW], F32, name="yt", bufs=3)
+                yt = work.tile([P, 2, CW], F32, name="yt", bufs=3)
                 tiles["Y", i] = yt
                 nc.vector.tensor_tensor(v3(y(i, 0)), v3(tiles["EB", i]), bc(xb, i), ALU.mult)
 
@@ -233,8 +261,21 @@ def tile_cn_pa_v_kernel(tc, x, cond, W1, b1, W2, b2, z1, p, num, den, grad_out, 
             def v_y2(i):
                 nc.vector.tensor_tensor(y(i, 1), tiles["EB", i], tiles["C", i], ALU.mult)
 
-            def v_s2(i):
-                nc.vector.scalar_tensor_tensor(y(i, 2), tiles["SB", i], -1.0, tiles["QA", i], ALU.add, ALU.add)
+            def first_of_later_tile(i):
+                return UNITS[i][0] > 0 and UNITS[i][1] == 0
+
+            def v_release(i):
+                w = UNITS[i][2] * LS
+                nc.scalar.copy(dp[:, 2 * SEC : 2 * SEC + w], tiles["H", i])
+
+            def v_dm2(i):
+                j, d0, n = UNITS[i]
+                if first_of_later_tile(i):
+                    tiles["H", i] = work.tile([P, CW], BF16, name="hold", bufs=1)[:, : n * LS]
+                    out = v3(tiles["H", i])
+                else:
+                    out = v3(dp[:, 2 * SEC + d0 * LS : 2 * SEC + (d0 + n) * LS])
+                nc.vector.scalar_tensor_tensor(out, v3(tiles["SB", i]), -1.0, bc(dd, i), ALU.add, ALU.mult)
 
             def v_last(j):
                 nc.vector.tensor_copy(dp[:, 3 * SEC :], last[:, j, :])
@@ -260,15 +301,15 @@ def tile_cn_pa_v_kernel(tc, x, cond, W1, b1, W2, b2, z1, p, num, den, grad_out, 
 
                 def quant():
                     if ("dpq", j) not in tiles:
-                        tiles["dpq", j] = work.tile([P, PASSES * P], U32, name="dpq", bufs=2, align_bytes=64)
-                        tiles["dps", j] = work.tile([P, PASSES * P], U8, name="dps", bufs=2, align_bytes=64)
+                        tiles["dpq", j] = work.tile([P, PASSES * P], U32, name="dpq", bufs=3, align_bytes=64)
+                        tiles["dps", j] = work.tile([P, PASSES * P], U8, name="dps", bufs=3, align_bytes=64)
                     cols = slice(slot * P, (slot + size) * P)
                     nc.vector.quantize_mx(out=tiles["dpq", j][:, cols].bitcast(E5M2), scales=tiles["dps", j][:, cols], in_=grp[:, : size * P * 4])
                     mx_ready.extend((j, slot + s) for s in range(size))
 
                 return quant
 
-            def turn_w2(g):
+            def turn_w2(g, late):
                 words = tiles["w2r", g][:].bitcast(F32)
                 grp = work.tile([P, HID * 4], BF16, name="w2g", bufs=2, align_bytes=64)
                 for half in range(2):
@@ -277,7 +318,10 @@ def tile_cn_pa_v_kernel(tc, x, cond, W1, b1, W2, b2, z1, p, num, den, grad_out, 
                         for u in range(2):
                             nc.tensor.transpose(bank[:, h, u, :], words[:, 2 * half + h, u:256:2], ident[:])
                     out = grp[:].bitcast(F32)[:, 512 * half : 512 * (half + 1)].rearrange("p (h r u) -> p h r u", h=2, u=2)
-                    nc.scalar.copy(out, bank[:].rearrange("p h u r -> p h r u"))
+                    if late is not None and half == 1:
+                        late.append(lambda out=out, bank=bank: copy_words("vector", out, bank[:].rearrange("p h u r -> p h r u")))
+                    else:
+                        copy_words("scalar", out, bank[:].rearrange("p h u r -> p h r u"))
 
                 def quant():
                     nc.vector.quantize_mx(out=w2q[:, g, :].bitcast(E4M3), scales=w2s[:, g, :], in_=grp[:])
@@ -307,7 +351,7 @@ def tile_cn_pa_v_kernel(tc, x, cond, W1, b1, W2, b2, z1, p, num, den, grad_out, 
                 return n == PASSES - 1
 
             def dz_mask(j):
-                nc.vector.scalar_tensor_tensor(dz[:, j, :], z1t[:, j, :], 0.0, tiles["acc", j][:], ALU.is_gt, ALU.mult)
+                nc.vector.scalar_tensor_tensor(dz[:, j, :], tiles["z1", j], 0.0, tiles["acc", j][:], ALU.is_gt, ALU.mult)
 
             def dz_turn(j):
                 words = dz[:, j, :].bitcast(F32)
@@ -352,40 +396,54 @@ def tile_cn_pa_v_kernel(tc, x, cond, W1, b1, W2, b2, z1, p, num, den, grad_out, 
             def cond_quant():
                 nc.vector.quantize_mx(out=cdq[:].bitcast(E4M3), scales=cds[:], in_=cdg[:].rearrange("p d j -> p (d j)"))
 
-            nc.vector.memset(sg[:, 0, 0:1], 0.0)
-            nc.scalar.activation(sg[:, 0, 0:1], sg[:, 0, 0:1], ACT.Sigmoid)
-            nc.scalar.activation(sg[:], ea[:, :, 0:DIM], ACT.Sigmoid, scale=0.1)
-            nc.scalar.activation(om[:], ea[:, :, 0:DIM], ACT.Sigmoid, scale=-0.1)
-            nc.scalar.activation(tt[:], ea[:, :, DIM:], ACT.Exp, scale=0.1)
+            nc.vector.memset(om[:, 0, 0:1], 0.0)
+            nc.scalar.activation(om[:, 0, 0:1], om[:, 0, 0:1], ACT.Exp)
+            nc.vector.tensor_copy(xf[:], xb[:])
 
             def has(i):
                 return 0 <= i < NU
 
             pend = []
             stage = {}
-            for k in range(-3, NU + 2):
+            late = []
+            for k in range(-3, NU + 1):
                 new = []
                 if has(k + 1):
-                    g_w(k + 1)
-                if has(k + 3):
-                    g_m(k + 3)
+                    make_w(k + 1)
+                if has(k):
+                    make_qa(k)
                 if has(k - 2):
                     s_out(k - 2)
+                if has(k + 3):
+                    make_m(k + 3)
+                if has(k - 2):
+                    if first_of_later_tile(k - 2):
+                        v_release(k - 2)
+                    for group in groups[k - 2]:
+                        new.append(turn_dp(UNITS[k - 2][0], group))
                 if has(k):
                     v_t1(k)
                     v_y2(k)
-                    v_s2(k)
+                if has(k - 1):
+                    v_dm2(k - 1)
                 if has(k + 1):
                     v_s1(k + 1)
+                for task in late:
+                    task()
+                if has(k + 1):
                     pe_back(k + 1)
                 if has(k + 2):
                     pe_z(k + 2)
                     s_exp(k + 2)
-                if has(k - 2):
-                    for n, group in enumerate(groups[k - 2]):
-                        new.append(turn_dp(UNITS[k - 2][0], group, "vector" if k == NU + 1 and n % 2 else "scalar"))
-                for g in w2_at.get(k, []):
-                    new.append(turn_w2(g))
+                if has(k):
+                    pe_sum(k)
+                if k == -1:
+                    nc.scalar.activation(tt[:], ea[:, :, DIM:], ACT.Exp, scale=0.1)
+                    nc.scalar.activation(sg[:], ea[:, :, 0:DIM], ACT.Sigmoid, scale=0.1)
+                    nc.scalar.activation(om[:], ea[:, :, 0:DIM], ACT.Sigmoid, scale=-0.1)
+                late = []
+                for n, g in enumerate(w2_at.get(k, [])):
+                    new.append(turn_w2(g, late if n == 0 else None))
                 if k == 2:
                     w1_turn()
                     new += [w1_quant, cond_group, cond_quant]
@@ -398,18 +456,25 @@ def tile_cn_pa_v_kernel(tc, x, cond, W1, b1, W2, b2, z1, p, num, den, grad_out, 
                         stage[j] = (k, "store")
 
                 ready_now = len(mx_ready)
+                w2_now = len(w2_done)
                 todo = []
                 if k == -2:
-                    todo.append(lambda: small_a(0, J))
+                    todo.append(lambda: small_r(0, 1))
                 if has(k + 1):
                     todo.append(lambda: v_q(k + 1))
                 if has(k - 1):
                     todo.append(lambda: v_y1(k - 1))
-                if has(k + 1):
-                    todo.append(lambda: v_qa(k + 1))
-                if k == -1:
+                if k == NU:
+                    todo.append(lambda: v_out(NU - 1))
+                if k == 0:
+                    todo.append(lambda: small_d(0, 1))
+                if k == 2:
+                    todo.append(lambda: small_r(1, J))
+                if k == 3:
+                    todo.append(lambda: small_d(1, J))
+                if k == 4:
                     todo.append(lambda: small_b(0, J))
-                if has(k) and UNITS[k][1] == SIZES[UNITS[k][0]][0]:
+                if has(k) and UNITS[k][1] == sum(SIZES[UNITS[k][0]][:5]):
                     todo.append(lambda: v_last(UNITS[k][0]))
                 slots = len(todo)
                 done = 0
@@ -433,38 +498,52 @@ def tile_cn_pa_v_kernel(tc, x, cond, W1, b1, W2, b2, z1, p, num, den, grad_out, 
                     nc.sync.dma_start(out=w1r[:], in_=W1)
                     nc.sync.dma_start(out=cdr[:], in_=rows(cond))
                 if k == 10:
-                    nc.sync.dma_start(out=z1t[:], in_=rows(z1))
+                    for j, name in enumerate(("dn", "sg", "om", "tt")):
+                        z1t = keep.tile([P, J, DIM], F32, name=name)
+                        tiles["z1", j] = z1t[:].rearrange("p a d -> p (a d)")
+                        nc.sync.dma_start(out=tiles["z1", j], in_=rows(z1)[:, j, :])
 
                 for j in range(J):
                     if stage.get(j) == (k - 1, "turn"):
                         dz_mx(j)
                         stage[j] = (k, "mx")
-                if len(w2_done) == PASSES:
-                    take = min(ready_now, PASSES)
-                    for j, s in mx_ready[:take]:
-                        if mx(j, s):
-                            pend.append(lambda j=j: dz_mask(j))
-                            stage[j] = (k + 1, "mask")
-                    mx_ready = mx_ready[take:]
+                now = [(j, s) for j, s in mx_ready[:ready_now] if slot_pass[j, s] in w2_done[:w2_now]]
+                now = [(j, s) for j, s in now if j < 2 or stage.get(j - 2, (0, ""))[1] == "store"][:MX_A_STEP]
+                for j, s in now:
+                    mx_ready.remove((j, s))
+                    if mx(j, s):
+                        pend.append(lambda j=j: dz_mask(j))
+                        stage[j] = (k + 1, "mask")
 
             for task in pend:
                 task()
+            tail = [turn_dp(J - 1, group, "vector" if n % 2 else "scalar") for n, group in enumerate(groups[NU - 1])]
             for j, s in mx_ready:
                 mx(j, s)
-            for j in range(J):
-                at = stage[j][1] if j in stage else "none"
-                if at == "none":
-                    dz_mask(j)
-                if at in ("none", "mask"):
+            mx_ready.clear()
+            for task in tail:
+                task()
+            for j, s in mx_ready:
+                mx(j, s)
+            for j in range(J - 1):
+                if stage[j][1] == "mask":
                     dz_turn(j)()
-                if at in ("none", "mask", "turn"):
+                if stage[j][1] in ("mask", "turn"):
                     dz_mx(j)
-                if at != "store":
+                if stage[j][1] != "store":
                     dz_store(j)
-            nc.vector.tensor_copy(dzi[:], dz[:].rearrange("p j h -> p h j"))
+            dz_mask(J - 1)
+            last_quant = dz_turn(J - 1)
+            cut = 320
+            dzi = keep.tile([P, HID, J], BF16, name="ea", align_bytes=64)
+            nc.vector.tensor_copy(dzi[:, :cut, :], dz[:, :, :cut].rearrange("p j h -> p h j"))
+            nc.scalar.copy(dzi[:, cut:, :], dz[:, :, cut:].rearrange("p j h -> p h j"))
+            last_quant()
             nc.vector.quantize_mx(out=dziq[:].bitcast(E5M2), scales=dzis[:], in_=dzi[:].rearrange("p h j -> p (h j)"))
+            dz_mx(J - 1)
             o1 = psum.tile([P, HID], F32, name="acc", bufs=2)
             nc.tensor.matmul_mx(out=o1[:], lhsT=cdq[:].bitcast(E4M3), lhsT_scale=cds[:], rhs=dziq[:].bitcast(E5M2), rhs_scale=dzis[:], start=True, stop=True)
+            dz_store(J - 1)
             ob1 = work.tile([P, HID], F32, name="ob1", bufs=1)
             nc.scalar.copy(ob1[:], o1[:])
             nc.sync.dma_start(out=out_1, in_=ob1[:])

@@ -21,11 +21,12 @@ PASS = 512
 PASSES = NCOL // PASS
 PC = 9216
 
-SIZES = [[8, 16, 22, 22, 20, 20, 20], [22, 22, 22, 22, 20, 20], [22, 22, 22, 22, 20, 20], [22, 22, 22, 22, 20, 12, 8]]
+SIZES = [[8, 16, 22, 22, 20, 20, 20], [22, 22, 22, 22, 20, 20], [22, 22, 22, 22, 20, 20], [22, 22, 22, 22, 14, 14, 12]]
 CW = max(max(s) for s in SIZES) * LS
 UNITS = [(j, sum(SIZES[j][:c]), n) for j in range(J) for c, n in enumerate(SIZES[j])]
 NU = len(UNITS)
 W2_STEPS = 16
+M_ON_SCALAR = 7
 MX_A_STEP = 9
 
 FLOPS = 2 * B * NCOL * HID + 2 * 2 * B * HID * DIM
@@ -83,6 +84,7 @@ def tile_cn_pa_v_kernel(tc, x, cond, W1, b1, W2, b2, z1, p, num, den, grad_out, 
 
         xb = keep.tile([P, J, DIM], BF16, name="xb")
         gb = keep.tile([P, J, DIM], BF16, name="gb")
+        nm = keep.tile([P, J, DIM], F32, name="nm")
         rr = keep.tile([P, J, DIM], F32, name="rr")
         dn = keep.tile([P, J, DIM], F32, name="dn")
         ea = keep.tile([P, J, 2 * DIM], F32, name="ea", align_bytes=64)
@@ -118,11 +120,11 @@ def tile_cn_pa_v_kernel(tc, x, cond, W1, b1, W2, b2, z1, p, num, den, grad_out, 
                 tiles[name, i] = t
 
             def load_w2(g):
-                t = work.tile([P, HID // P, PASS], BF16, name="w2r", bufs=3, align_bytes=64)
+                t = work.tile([P, HID // P, PASS], BF16, name="w2r", bufs=2, align_bytes=64)
                 nc.sync.dma_start(out=t[:], in_=W2.rearrange("(h q) k -> q h k", q=P)[:, :, PASS * g : PASS * (g + 1)])
                 tiles["w2r", g] = t
 
-            pairs_in = ((dn, rows(den)), (rr, rows(num)), (ea, rows(p)[:, :, PC - 2 * DIM :]), (gb, rows(grad_out)))
+            pairs_in = ((dn, rows(den)), (nm, rows(num)), (ea, rows(p)[:, :, PC - 2 * DIM :]), (gb, rows(grad_out)))
             nc.sync.dma_start(out=xb[:], in_=rows(x))
             load("A", 0)
             load("C", 0)
@@ -141,7 +143,7 @@ def tile_cn_pa_v_kernel(tc, x, cond, W1, b1, W2, b2, z1, p, num, den, grad_out, 
 
             def small_r(a, b):
                 nc.vector.reciprocal(dn[:, a:b], dn[:, a:b])
-                nc.vector.tensor_tensor(rr[:, a:b], rr[:, a:b], dn[:, a:b], ALU.mult)
+                nc.vector.tensor_tensor(rr[:, a:b], nm[:, a:b], dn[:, a:b], ALU.mult)
 
             def small_d(a, b):
                 nc.vector.tensor_tensor(tt[:, a:b], gb[:, a:b], tt[:, a:b], ALU.mult)
@@ -151,12 +153,11 @@ def tile_cn_pa_v_kernel(tc, x, cond, W1, b1, W2, b2, z1, p, num, den, grad_out, 
             def small_b(a, b):
                 v = nc.vector
                 c0, c1 = ea[:, a:b, 0:DIM], ea[:, a:b, DIM:]
-                v.tensor_tensor(sg[:, a:b], sg[:, a:b], rr[:, a:b], ALU.mult)
+                v.scalar_tensor_tensor(c0, dd[:, a:b], 0.1, nm[:, a:b], ALU.mult, ALU.mult)
                 v.tensor_copy(last[:, a:b, 0:DIM], gb[:, a:b])
-                v.scalar_tensor_tensor(c0, sg[:, a:b], 0.8, xb[:, a:b], ALU.mult, ALU.add)
-                v.scalar_tensor_tensor(c1, tt[:, a:b], 0.08, sg[:, a:b], ALU.mult, ALU.mult)
-                v.scalar_tensor_tensor(last[:, a:b, 2 * DIM :], tt[:, a:b], 0.1, c0, ALU.mult, ALU.mult)
-                v.tensor_tensor(last[:, a:b, DIM : 2 * DIM], c1, om[:, a:b], ALU.mult)
+                v.scalar_tensor_tensor(c1, tt[:, a:b], 0.1, xb[:, a:b], ALU.mult, ALU.mult)
+                v.tensor_tensor(last[:, a:b, DIM : 2 * DIM], c0, om[:, a:b], ALU.mult)
+                v.tensor_tensor(last[:, a:b, 2 * DIM :], c1, c0, ALU.add)
 
             def bc(t, i, n=None):
                 j, d0, size = UNITS[i]
@@ -167,7 +168,7 @@ def tile_cn_pa_v_kernel(tc, x, cond, W1, b1, W2, b2, z1, p, num, den, grad_out, 
                 j, d0, n = UNITS[i]
                 out = dp[:, : 3 * SEC].rearrange("p (s w) -> p s w", s=3)[:, :, d0 * LS : (d0 + n) * LS].rearrange("p s (d l) -> p s d l", l=LS)
                 src = tiles["Y", i][:, :, : n * LS].rearrange("p s (d l) -> p s d l", l=LS)
-                for s in range(2):
+                for s in range(3):
                     nc.vector.tensor_tensor(out[:, s], src[:, s], bc(dd, i), ALU.mult)
 
             def v3(t):
@@ -183,8 +184,11 @@ def tile_cn_pa_v_kernel(tc, x, cond, W1, b1, W2, b2, z1, p, num, den, grad_out, 
 
             def make_m(i):
                 j, d0, n = UNITS[i]
+                ng = 0 if i < 3 else n - min(n, M_ON_SCALAR)
                 m, a = new_tile("M", i, 3), tiles["A", i]
-                for d in range(n):
+                if ng:
+                    nc.gpsimd.tensor_tensor(v3(m[:, : ng * LS]), v3(a[:, : ng * LS]), bc(xb, i, ng), ALU.mult)
+                for d in range(ng, n):
                     run = slice(d * LS, (d + 1) * LS)
                     nc.scalar.activation(m[:, run], a[:, run], ACT.Copy, scale=xf[:, j, d0 + d : d0 + d + 1])
 
@@ -212,25 +216,18 @@ def tile_cn_pa_v_kernel(tc, x, cond, W1, b1, W2, b2, z1, p, num, den, grad_out, 
                 tiles["ST", i] = st
                 nc.vector.scalar_tensor_tensor(st[:, :nb, :], tiles["ZT", i][:, :nb, :], 0.0, tiles["ET", i][:, :nb, :], ALU.max, ALU.add)
 
-            def pe_back(i):
-                bank = psum.tile([P, HID], F32, name="eb", bufs=1)
-                tiles["EB", i] = bank[:, : UNITS[i][2] * LS]
+            def pe_back(i, src, dst, bufs):
+                bank = psum.tile([P, HID], F32, name="b" + dst, bufs=bufs)
+                tiles[dst, i] = bank[:, : UNITS[i][2] * LS]
                 for b, c in enumerate(blocks(i)):
-                    nc.tensor.transpose(bank[:, c : c + P], tiles["ET", i][:, b, :], ident[:])
-
-            def pe_sum(i):
-                bank = psum.tile([P, HID], F32, name="sb", bufs=1)
-                tiles["SB", i] = bank[:, : UNITS[i][2] * LS]
-                for b, c in enumerate(blocks(i)):
-                    nc.tensor.matmul(bank[:, c : c + P], lhsT=tiles["ST", i][:, b, :], rhs=ident[:], is_transpose=True, start=True, stop=False)
-                    nc.tensor.matmul(bank[:, c : c + P], lhsT=ident[:], rhs=tiles["QA", i][:, c : c + P], start=False, stop=True)
+                    nc.tensor.transpose(bank[:, c : c + P], tiles[src, i][:, b, :], ident[:])
 
             def s_out(i):
                 j, d0, n = UNITS[i]
                 out = dp[:, : 3 * SEC].rearrange("p (s w) -> p s w", s=3)
                 for d in range(n):
                     nc.scalar.activation(
-                        out[:, 0:2, (d0 + d) * LS : (d0 + d + 1) * LS],
+                        out[:, :, (d0 + d) * LS : (d0 + d + 1) * LS],
                         tiles["Y", i][:, :, d * LS : (d + 1) * LS],
                         ACT.Copy,
                         scale=dd[:, j, d0 + d : d0 + d + 1],
@@ -243,12 +240,11 @@ def tile_cn_pa_v_kernel(tc, x, cond, W1, b1, W2, b2, z1, p, num, den, grad_out, 
                 w = v3(tiles["W", i])
                 nc.vector.scalar_tensor_tensor(w, w, 0.0, bc(rr, i), ALU.is_lt, ALU.mult)
 
-            def make_qa(i):
-                engine = nc.vector if i < 1 else nc.gpsimd
-                engine.tensor_tensor(new_tile("QA", i, 2), tiles["W", i], tiles["A", i], ALU.mult)
+            def v_qa(i):
+                nc.vector.tensor_tensor(new_tile("QA", i, 2), tiles["W", i], tiles["A", i], ALU.mult)
 
             def v_t1(i):
-                yt = work.tile([P, 2, CW], F32, name="yt", bufs=3)
+                yt = work.tile([P, 3, CW], F32, name="yt", bufs=3)
                 tiles["Y", i] = yt
                 nc.vector.tensor_tensor(v3(y(i, 0)), v3(tiles["EB", i]), bc(xb, i), ALU.mult)
 
@@ -261,21 +257,8 @@ def tile_cn_pa_v_kernel(tc, x, cond, W1, b1, W2, b2, z1, p, num, den, grad_out, 
             def v_y2(i):
                 nc.vector.tensor_tensor(y(i, 1), tiles["EB", i], tiles["C", i], ALU.mult)
 
-            def first_of_later_tile(i):
-                return UNITS[i][0] > 0 and UNITS[i][1] == 0
-
-            def v_release(i):
-                w = UNITS[i][2] * LS
-                nc.scalar.copy(dp[:, 2 * SEC : 2 * SEC + w], tiles["H", i])
-
-            def v_dm2(i):
-                j, d0, n = UNITS[i]
-                if first_of_later_tile(i):
-                    tiles["H", i] = work.tile([P, CW], BF16, name="hold", bufs=1)[:, : n * LS]
-                    out = v3(tiles["H", i])
-                else:
-                    out = v3(dp[:, 2 * SEC + d0 * LS : 2 * SEC + (d0 + n) * LS])
-                nc.vector.scalar_tensor_tensor(out, v3(tiles["SB", i]), -1.0, bc(dd, i), ALU.add, ALU.mult)
+            def v_s2(i):
+                nc.vector.scalar_tensor_tensor(y(i, 2), tiles["SB", i], -1.0, tiles["QA", i], ALU.add, ALU.add)
 
             def v_last(j):
                 nc.vector.tensor_copy(dp[:, 3 * SEC :], last[:, j, :])
@@ -290,7 +273,7 @@ def tile_cn_pa_v_kernel(tc, x, cond, W1, b1, W2, b2, z1, p, num, den, grad_out, 
                 slot, passes = group
                 size = len(passes)
                 words = dp[:].bitcast(F32)
-                grp = work.tile([P, 4 * P * 4], BF16, name="dpg", bufs=3, align_bytes=64)
+                grp = work.tile([P, 4 * P * 4], BF16, name="dpg", bufs=2, align_bytes=64)
                 for half in range(0, size, 2):
                     bank = psum.tile([P, 2, 2, P], F32, name="tr", bufs=3)
                     for h, g in enumerate(passes[half : half + 2]):
@@ -301,8 +284,8 @@ def tile_cn_pa_v_kernel(tc, x, cond, W1, b1, W2, b2, z1, p, num, den, grad_out, 
 
                 def quant():
                     if ("dpq", j) not in tiles:
-                        tiles["dpq", j] = work.tile([P, PASSES * P], U32, name="dpq", bufs=3, align_bytes=64)
-                        tiles["dps", j] = work.tile([P, PASSES * P], U8, name="dps", bufs=3, align_bytes=64)
+                        tiles["dpq", j] = work.tile([P, PASSES * P], U32, name="dpq", bufs=2, align_bytes=64)
+                        tiles["dps", j] = work.tile([P, PASSES * P], U8, name="dps", bufs=2, align_bytes=64)
                     cols = slice(slot * P, (slot + size) * P)
                     nc.vector.quantize_mx(out=tiles["dpq", j][:, cols].bitcast(E5M2), scales=tiles["dps", j][:, cols], in_=grp[:, : size * P * 4])
                     mx_ready.extend((j, slot + s) for s in range(size))
@@ -410,40 +393,35 @@ def tile_cn_pa_v_kernel(tc, x, cond, W1, b1, W2, b2, z1, p, num, den, grad_out, 
                 new = []
                 if has(k + 1):
                     make_w(k + 1)
-                if has(k):
-                    make_qa(k)
                 if has(k - 2):
                     s_out(k - 2)
-                if has(k + 3):
-                    make_m(k + 3)
-                if has(k - 2):
-                    if first_of_later_tile(k - 2):
-                        v_release(k - 2)
-                    for group in groups[k - 2]:
-                        new.append(turn_dp(UNITS[k - 2][0], group))
+                if has(k + 1):
+                    v_s1(k + 1)
                 if has(k):
                     v_t1(k)
                     v_y2(k)
-                if has(k - 1):
-                    v_dm2(k - 1)
-                if has(k + 1):
-                    v_s1(k + 1)
+                    v_s2(k)
                 for task in late:
                     task()
-                if has(k + 1):
-                    pe_back(k + 1)
                 if has(k + 2):
                     pe_z(k + 2)
                     s_exp(k + 2)
-                if has(k):
-                    pe_sum(k)
+                if has(k + 1):
+                    pe_back(k + 1, "ET", "EB", 1)
+                if has(k + 1):
+                    pe_back(k + 1, "ST", "SB", 1)
+                if has(k - 2):
+                    for group in groups[k - 2]:
+                        new.append(turn_dp(UNITS[k - 2][0], group))
+                if has(k + 3):
+                    make_m(k + 3)
                 if k == -1:
                     nc.scalar.activation(tt[:], ea[:, :, DIM:], ACT.Exp, scale=0.1)
                     nc.scalar.activation(sg[:], ea[:, :, 0:DIM], ACT.Sigmoid, scale=0.1)
                     nc.scalar.activation(om[:], ea[:, :, 0:DIM], ACT.Sigmoid, scale=-0.1)
                 late = []
                 for n, g in enumerate(w2_at.get(k, [])):
-                    new.append(turn_w2(g, late if n == 0 else None))
+                    new.append(turn_w2(g, None))
                 if k == 2:
                     w1_turn()
                     new += [w1_quant, cond_group, cond_quant]
@@ -466,6 +444,8 @@ def tile_cn_pa_v_kernel(tc, x, cond, W1, b1, W2, b2, z1, p, num, den, grad_out, 
                     todo.append(lambda: v_y1(k - 1))
                 if k == NU:
                     todo.append(lambda: v_out(NU - 1))
+                if has(k + 1):
+                    todo.append(lambda: v_qa(k + 1))
                 if k == 0:
                     todo.append(lambda: small_d(0, 1))
                 if k == 2:

from contextlib import ExitStack

import concourse.mybir as mybir
from concourse.masks import make_identity

F32 = mybir.dt.float32
BF16 = mybir.dt.bfloat16
U32 = mybir.dt.uint32
U8 = mybir.dt.uint8
E4M3 = mybir.dt.float8_e4m3fn_x4
E5M2 = mybir.dt.float8_e5m2_x4
ALU = mybir.AluOpType
ACT = mybir.ActivationFunctionType

P = 128
B, DIM, HID, LS = 512, 128, 512, 23
J = B // P
SEC = DIM * LS
NCOL = 3 * SEC + 3 * DIM
PASS = 512
PASSES = NCOL // PASS
PC = 9216

SIZES = [[8, 16, 22, 22, 20, 20, 20], [22, 22, 22, 22, 20, 20], [22, 22, 22, 22, 20, 20], [22, 22, 22, 22, 14, 14, 12]]
CW = max(max(s) for s in SIZES) * LS
UNITS = [(j, sum(SIZES[j][:c]), n) for j in range(J) for c, n in enumerate(SIZES[j])]
NU = len(UNITS)
W2_STEPS = 16
M_ON_SCALAR = 7
MX_A_STEP = 9

FLOPS = 2 * B * NCOL * HID + 2 * 2 * B * HID * DIM
BYTES = B * (PC - DIM) * 4 + HID * PC * 2 + 3 * B * DIM * 2 + DIM * HID * 2 + B * HID * 4 + 2 * B * DIM * 4 + 2 * B * DIM * 4


def groups_by_unit():
    result = []
    for j in range(J):
        ends = [sum(SIZES[j][: c + 1]) * LS for c in range(len(SIZES[j]))]

        def chunk(k):
            return min(c for c in range(len(ends)) if k % SEC < ends[c]) if k < 3 * SEC else 0

        ready = [max(chunk(k) for k in range(PASS * g, PASS * (g + 1))) for g in range(PASSES)]
        size = 4 if j < J - 1 else 2
        waiting = []
        slot = 0
        for c in range(len(ends)):
            groups = []
            waiting += [g for g in range(PASSES) if ready[g] == c]
            while len(waiting) >= size or (waiting and c == len(ends) - 1):
                groups.append((slot, waiting[:size]))
                slot += len(waiting[:size])
                waiting = waiting[size:]
            result.append(groups)
    return result


def tile_cn_pa_v_kernel(tc, x, cond, W1, b1, W2, b2, z1, p, num, den, grad_out, out_0, out_1):
    nc = tc.nc
    groups = groups_by_unit()
    slot_pass = {}
    for i, (j, d0, n) in enumerate(UNITS):
        for slot, passes in groups[i]:
            for s, g in enumerate(passes):
                slot_pass[j, slot + s] = g
    w2_order = [slot_pass[0, s] for s in range(PASSES)]
    w2_at = {k: w2_order[k * PASSES // W2_STEPS : (k + 1) * PASSES // W2_STEPS] for k in range(W2_STEPS)}

    def rows(ap):
        return ap.rearrange("(p j) w -> p j w", j=J)

    with ExitStack() as ctx:
        keep = ctx.enter_context(tc.tile_pool(name="keep", bufs=1))
        work = ctx.enter_context(tc.tile_pool(name="work", bufs=2))
        psum = ctx.enter_context(tc.psum_pool(name="psum", bufs=1))

        ident = keep.tile([P, P], F32, name="ident")
        make_identity(nc, ident[:])
        w1q = keep.tile([P, HID], U32, name="w1q", align_bytes=64)
        w1s = keep.tile([P, HID], U8, name="w1s", align_bytes=64)
        nc.gpsimd.memset(w1q[:, DIM:], 0)
        nc.gpsimd.memset(w1s[:, DIM:], 0)

        xb = keep.tile([P, J, DIM], BF16, name="xb")
        gb = keep.tile([P, J, DIM], BF16, name="gb")
        nm = keep.tile([P, J, DIM], F32, name="nm")
        rr = keep.tile([P, J, DIM], F32, name="rr")
        dn = keep.tile([P, J, DIM], F32, name="dn")
        ea = keep.tile([P, J, 2 * DIM], F32, name="ea", align_bytes=64)
        xf = keep.tile([P, J, DIM], F32, name="xf")
        sg = keep.tile([P, J, DIM], F32, name="sg")
        om = keep.tile([P, J, DIM], F32, name="om")
        tt = keep.tile([P, J, DIM], F32, name="tt")
        dd = keep.tile([P, J, DIM], F32, name="dd")
        last = keep.tile([P, J, 3 * DIM], BF16, name="last")
        dp = keep.tile([P, NCOL], BF16, name="dp", align_bytes=64)
        w2q = keep.tile([P, PASSES, HID], U32, name="w2q", align_bytes=64)
        w2s = keep.tile([P, PASSES, HID], U8, name="w2s", align_bytes=64)
        dz = keep.tile([P, J, HID], BF16, name="dz", align_bytes=64)
        w1r = keep.tile([P, HID], BF16, name="w1r", align_bytes=64)
        w1g = keep.tile([P, HID], BF16, name="w1g", align_bytes=64)
        cdr = keep.tile([P, J, DIM], BF16, name="cdr")
        cdg = keep.tile([P, DIM, J], BF16, name="cdg", align_bytes=64)
        cdq = keep.tile([P, DIM], U32, name="cdq", align_bytes=64)
        cds = keep.tile([P, DIM], U8, name="cds", align_bytes=64)
        dziq = keep.tile([P, HID], U32, name="dziq", align_bytes=64)
        dzis = keep.tile([P, HID], U8, name="dzis", align_bytes=64)

        with tc.manual_schedule():
            tiles = {}

            def load(name, i):
                if (name, i) in tiles or not 0 <= i < NU:
                    return
                sec, bufs = {"A": (0, 5), "B": (1, 3), "C": (2, 5)}[name]
                j, d0, n = UNITS[i]
                t = work.tile([P, CW], F32, name="in" + name, bufs=bufs)[:, : n * LS]
                nc.sync.dma_start(out=t, in_=rows(p)[:, j, sec * SEC + d0 * LS : sec * SEC + (d0 + n) * LS])
                tiles[name, i] = t

            def load_w2(g):
                t = work.tile([P, HID // P, PASS], BF16, name="w2r", bufs=2, align_bytes=64)
                nc.sync.dma_start(out=t[:], in_=W2.rearrange("(h q) k -> q h k", q=P)[:, :, PASS * g : PASS * (g + 1)])
                tiles["w2r", g] = t

            pairs_in = ((dn, rows(den)), (nm, rows(num)), (ea, rows(p)[:, :, PC - 2 * DIM :]), (gb, rows(grad_out)))
            nc.sync.dma_start(out=xb[:], in_=rows(x))
            load("A", 0)
            load("C", 0)
            load("B", 0)
            for t, src in pairs_in[:2]:
                nc.sync.dma_start(out=t[:, 0:1], in_=src[:, 0:1])
            load("A", 1)
            load("C", 1)
            load("B", 1)
            load("A", 2)
            for t, src in pairs_in[2:]:
                nc.sync.dma_start(out=t[:], in_=src)
            load("B", 2)
            for t, src in pairs_in[:2]:
                nc.sync.dma_start(out=t[:, 1:], in_=src[:, 1:])

            def small_r(a, b):
                nc.vector.reciprocal(dn[:, a:b], dn[:, a:b])
                nc.vector.tensor_tensor(rr[:, a:b], nm[:, a:b], dn[:, a:b], ALU.mult)

            def small_d(a, b):
                nc.vector.tensor_tensor(tt[:, a:b], gb[:, a:b], tt[:, a:b], ALU.mult)
                nc.vector.tensor_tensor(dn[:, a:b], sg[:, a:b], dn[:, a:b], ALU.mult)
                nc.vector.scalar_tensor_tensor(dd[:, a:b], tt[:, a:b], 0.8, dn[:, a:b], ALU.mult, ALU.mult)

            def small_b(a, b):
                v = nc.vector
                c0, c1 = ea[:, a:b, 0:DIM], ea[:, a:b, DIM:]
                v.scalar_tensor_tensor(c0, dd[:, a:b], 0.1, nm[:, a:b], ALU.mult, ALU.mult)
                v.tensor_copy(last[:, a:b, 0:DIM], gb[:, a:b])
                v.scalar_tensor_tensor(c1, tt[:, a:b], 0.1, xb[:, a:b], ALU.mult, ALU.mult)
                v.tensor_tensor(last[:, a:b, DIM : 2 * DIM], c0, om[:, a:b], ALU.mult)
                v.tensor_tensor(last[:, a:b, 2 * DIM :], c1, c0, ALU.add)

            def bc(t, i, n=None):
                j, d0, size = UNITS[i]
                n = size if n is None else n
                return t[:, j, d0 : d0 + n].unsqueeze(2).to_broadcast([P, n, LS])

            def v_out(i):
                j, d0, n = UNITS[i]
                out = dp[:, : 3 * SEC].rearrange("p (s w) -> p s w", s=3)[:, :, d0 * LS : (d0 + n) * LS].rearrange("p s (d l) -> p s d l", l=LS)
                src = tiles["Y", i][:, :, : n * LS].rearrange("p s (d l) -> p s d l", l=LS)
                for s in range(3):
                    nc.vector.tensor_tensor(out[:, s], src[:, s], bc(dd, i), ALU.mult)

            def v3(t):
                return t.rearrange("p (d l) -> p d l", l=LS)

            def new_tile(key, i, bufs):
                tiles[key, i] = work.tile([P, CW], F32, name="t" + key, bufs=bufs)[:, : UNITS[i][2] * LS]
                return tiles[key, i]

            def blocks(i):
                w = UNITS[i][2] * LS
                return [min(P * b, w - P) for b in range((w + P - 1) // P)]

            def make_m(i):
                j, d0, n = UNITS[i]
                ng = 0 if i < 3 else n - min(n, M_ON_SCALAR)
                m, a = new_tile("M", i, 3), tiles["A", i]
                if ng:
                    nc.gpsimd.tensor_tensor(v3(m[:, : ng * LS]), v3(a[:, : ng * LS]), bc(xb, i, ng), ALU.mult)
                for d in range(ng, n):
                    run = slice(d * LS, (d + 1) * LS)
                    nc.scalar.activation(m[:, run], a[:, run], ACT.Copy, scale=xf[:, j, d0 + d : d0 + d + 1])

            def make_w(i):
                engine = nc.vector if i < 2 else nc.gpsimd
                engine.tensor_tensor(new_tile("W", i, 2), tiles["A", i], tiles["C", i], ALU.mult)

            def pe_z(i):
                zt = psum.tile([P, 4, P], F32, name="zt", bufs=1)
                tiles["ZT", i] = zt
                for b, c in enumerate(blocks(i)):
                    nc.tensor.matmul(zt[:, b, :], lhsT=tiles["M", i][:, c : c + P], rhs=ident[:], is_transpose=True, start=True, stop=False)
                    nc.tensor.matmul(zt[:, b, :], lhsT=tiles["B", i][:, c : c + P], rhs=ident[:], is_transpose=True, start=False, stop=True)

            def s_exp(i):
                nb = len(blocks(i))
                et = work.tile([P, 4, P], F32, name="et", bufs=2)
                tiles["ET", i] = et
                nc.scalar.activation(et[:, :nb, :], tiles["ZT", i][:, :nb, :], ACT.Relu, scale=-1.0)
                nc.scalar.activation(et[:, :nb, :], et[:, :nb, :], ACT.Exp, scale=-1.0)

            def v_s1(i):
                nb = len(blocks(i))
                st = work.tile([P, 4, P], F32, name="st", bufs=3)
                tiles["ST", i] = st
                nc.vector.scalar_tensor_tensor(st[:, :nb, :], tiles["ZT", i][:, :nb, :], 0.0, tiles["ET", i][:, :nb, :], ALU.max, ALU.add)

            def pe_back(i, src, dst, bufs):
                bank = psum.tile([P, HID], F32, name="b" + dst, bufs=bufs)
                tiles[dst, i] = bank[:, : UNITS[i][2] * LS]
                for b, c in enumerate(blocks(i)):
                    nc.tensor.transpose(bank[:, c : c + P], tiles[src, i][:, b, :], ident[:])

            def s_out(i):
                j, d0, n = UNITS[i]
                out = dp[:, : 3 * SEC].rearrange("p (s w) -> p s w", s=3)
                for d in range(n):
                    nc.scalar.activation(
                        out[:, :, (d0 + d) * LS : (d0 + d + 1) * LS],
                        tiles["Y", i][:, :, d * LS : (d + 1) * LS],
                        ACT.Copy,
                        scale=dd[:, j, d0 + d : d0 + d + 1],
                    )

            def y(i, s):
                return tiles["Y", i][:, s, : UNITS[i][2] * LS]

            def v_q(i):
                w = v3(tiles["W", i])
                nc.vector.scalar_tensor_tensor(w, w, 0.0, bc(rr, i), ALU.is_lt, ALU.mult)

            def v_qa(i):
                nc.vector.tensor_tensor(new_tile("QA", i, 2), tiles["W", i], tiles["A", i], ALU.mult)

            def v_t1(i):
                yt = work.tile([P, 3, CW], F32, name="yt", bufs=3)
                tiles["Y", i] = yt
                nc.vector.tensor_tensor(v3(y(i, 0)), v3(tiles["EB", i]), bc(xb, i), ALU.mult)

            def v_t2(i):
                nc.vector.tensor_tensor(y(i, 0), y(i, 0), tiles["W", i], ALU.add)

            def v_y1(i):
                nc.vector.tensor_tensor(y(i, 0), y(i, 0), tiles["C", i], ALU.mult)

            def v_y2(i):
                nc.vector.tensor_tensor(y(i, 1), tiles["EB", i], tiles["C", i], ALU.mult)

            def v_s2(i):
                nc.vector.scalar_tensor_tensor(y(i, 2), tiles["SB", i], -1.0, tiles["QA", i], ALU.add, ALU.add)

            def v_last(j):
                nc.vector.tensor_copy(dp[:, 3 * SEC :], last[:, j, :])

            def copy_words(engine, out, bank):
                if engine == "vector":
                    nc.vector.tensor_copy(out, bank)
                else:
                    nc.scalar.copy(out, bank)

            def turn_dp(j, group, engine="scalar"):
                slot, passes = group
                size = len(passes)
                words = dp[:].bitcast(F32)
                grp = work.tile([P, 4 * P * 4], BF16, name="dpg", bufs=2, align_bytes=64)
                for half in range(0, size, 2):
                    bank = psum.tile([P, 2, 2, P], F32, name="tr", bufs=3)
                    for h, g in enumerate(passes[half : half + 2]):
                        for u in range(2):
                            nc.tensor.transpose(bank[:, h, u, :], words[:, 256 * g + u : 256 * (g + 1) : 2], ident[:])
                    out = grp[:].bitcast(F32)[:, half * 256 : half * 256 + 512].rearrange("p (h r u) -> p h r u", h=2, u=2)
                    copy_words(engine, out, bank[:].rearrange("p h u r -> p h r u"))

                def quant():
                    if ("dpq", j) not in tiles:
                        tiles["dpq", j] = work.tile([P, PASSES * P], U32, name="dpq", bufs=2, align_bytes=64)
                        tiles["dps", j] = work.tile([P, PASSES * P], U8, name="dps", bufs=2, align_bytes=64)
                    cols = slice(slot * P, (slot + size) * P)
                    nc.vector.quantize_mx(out=tiles["dpq", j][:, cols].bitcast(E5M2), scales=tiles["dps", j][:, cols], in_=grp[:, : size * P * 4])
                    mx_ready.extend((j, slot + s) for s in range(size))

                return quant

            def turn_w2(g, late):
                words = tiles["w2r", g][:].bitcast(F32)
                grp = work.tile([P, HID * 4], BF16, name="w2g", bufs=2, align_bytes=64)
                for half in range(2):
                    bank = psum.tile([P, 2, 2, P], F32, name="tr", bufs=3)
                    for h in range(2):
                        for u in range(2):
                            nc.tensor.transpose(bank[:, h, u, :], words[:, 2 * half + h, u:256:2], ident[:])
                    out = grp[:].bitcast(F32)[:, 512 * half : 512 * (half + 1)].rearrange("p (h r u) -> p h r u", h=2, u=2)
                    if late is not None and half == 1:
                        late.append(lambda out=out, bank=bank: copy_words("vector", out, bank[:].rearrange("p h u r -> p h r u")))
                    else:
                        copy_words("scalar", out, bank[:].rearrange("p h u r -> p h r u"))

                def quant():
                    nc.vector.quantize_mx(out=w2q[:, g, :].bitcast(E4M3), scales=w2s[:, g, :], in_=grp[:])
                    w2_done.append(g)

                return quant

            mx_ready = []
            w2_done = []

            def mx(j, s):
                if ("acc", j) not in tiles:
                    tiles["acc", j] = psum.tile([P, HID], F32, name="acc", bufs=2)
                    tiles["n", j] = 0
                g = slot_pass[j, s]
                n = tiles["n", j]
                nc.tensor.matmul_mx(
                    out=tiles["acc", j][:],
                    lhsT=tiles["dpq", j][:, s * P : (s + 1) * P].bitcast(E5M2),
                    lhsT_scale=tiles["dps", j][:, s * P : (s + 1) * P],
                    rhs=w2q[:, g, :].bitcast(E4M3),
                    rhs_scale=w2s[:, g, :],
                    start=(n == 0),
                    stop=(n == PASSES - 1),
                )
                tiles["n", j] = n + 1
                return n == PASSES - 1

            def dz_mask(j):
                nc.vector.scalar_tensor_tensor(dz[:, j, :], tiles["z1", j], 0.0, tiles["acc", j][:], ALU.is_gt, ALU.mult)

            def dz_turn(j):
                words = dz[:, j, :].bitcast(F32)
                bank = psum.tile([P, 2, P], F32, name="tr", bufs=3)
                for u in range(2):
                    nc.tensor.transpose(bank[:, u, :], words[:, u:256:2], ident[:])
                grp = work.tile([P, P * 4], BF16, name="dzg", bufs=2, align_bytes=64)
                nc.scalar.copy(grp[:].bitcast(F32).rearrange("p (r u) -> p r u", u=2), bank[:].rearrange("p u r -> p r u"))

                def quant():
                    q = work.tile([P, P], U32, name="dzq", bufs=2, align_bytes=64)
                    sc = work.tile([P, P], U8, name="dzs", bufs=2, align_bytes=64)
                    nc.vector.quantize_mx(out=q[:].bitcast(E5M2), scales=sc[:], in_=grp[:])
                    tiles["dzq", j] = (q, sc)

                return quant

            def dz_mx(j):
                q, sc = tiles["dzq", j]
                o = psum.tile([P, HID], F32, name="acc", bufs=2)
                nc.tensor.matmul_mx(out=o[:], lhsT=q[:].bitcast(E5M2), lhsT_scale=sc[:], rhs=w1q[:].bitcast(E4M3), rhs_scale=w1s[:], start=True, stop=True)
                tiles["o", j] = o

            def dz_store(j):
                ob = work.tile([P, DIM], F32, name="ob", bufs=2)
                nc.scalar.copy(ob[:], tiles["o", j][:, 0:DIM])
                nc.sync.dma_start(out=rows(out_0)[:, j, :], in_=ob[:])

            def w1_turn():
                words = w1r[:].bitcast(F32)
                bank = psum.tile([P, 2, P], F32, name="tr", bufs=3)
                for u in range(2):
                    nc.tensor.transpose(bank[:, u, :], words[:, u:256:2], ident[:])
                nc.scalar.copy(w1g[:].bitcast(F32).rearrange("p (r u) -> p r u", u=2), bank[:].rearrange("p u r -> p r u"))

            def w1_quant():
                nc.vector.quantize_mx(out=w1q[:, 0:DIM].bitcast(E4M3), scales=w1s[:, 0:DIM], in_=w1g[:])

            def cond_group():
                nc.vector.tensor_copy(cdg[:], cdr[:].rearrange("p j d -> p d j"))

            def cond_quant():
                nc.vector.quantize_mx(out=cdq[:].bitcast(E4M3), scales=cds[:], in_=cdg[:].rearrange("p d j -> p (d j)"))

            nc.vector.memset(om[:, 0, 0:1], 0.0)
            nc.scalar.activation(om[:, 0, 0:1], om[:, 0, 0:1], ACT.Exp)
            nc.vector.tensor_copy(xf[:], xb[:])

            def has(i):
                return 0 <= i < NU

            pend = []
            stage = {}
            late = []
            for k in range(-3, NU + 1):
                new = []
                if has(k + 1):
                    make_w(k + 1)
                if has(k - 2):
                    s_out(k - 2)
                if has(k + 1):
                    v_s1(k + 1)
                if has(k):
                    v_t1(k)
                    v_y2(k)
                    v_s2(k)
                for task in late:
                    task()
                if has(k + 2):
                    pe_z(k + 2)
                    s_exp(k + 2)
                if has(k + 1):
                    pe_back(k + 1, "ET", "EB", 1)
                if has(k + 1):
                    pe_back(k + 1, "ST", "SB", 1)
                if has(k - 2):
                    for group in groups[k - 2]:
                        new.append(turn_dp(UNITS[k - 2][0], group))
                if has(k + 3):
                    make_m(k + 3)
                if k == -1:
                    nc.scalar.activation(tt[:], ea[:, :, DIM:], ACT.Exp, scale=0.1)
                    nc.scalar.activation(sg[:], ea[:, :, 0:DIM], ACT.Sigmoid, scale=0.1)
                    nc.scalar.activation(om[:], ea[:, :, 0:DIM], ACT.Sigmoid, scale=-0.1)
                late = []
                for n, g in enumerate(w2_at.get(k, [])):
                    new.append(turn_w2(g, None))
                if k == 2:
                    w1_turn()
                    new += [w1_quant, cond_group, cond_quant]
                for j in range(J):
                    if stage.get(j) == (k - 1, "mask"):
                        new.append(dz_turn(j))
                        stage[j] = (k, "turn")
                    elif stage.get(j) == (k - 1, "mx"):
                        dz_store(j)
                        stage[j] = (k, "store")

                ready_now = len(mx_ready)
                w2_now = len(w2_done)
                todo = []
                if k == -2:
                    todo.append(lambda: small_r(0, 1))
                if has(k + 1):
                    todo.append(lambda: v_q(k + 1))
                if has(k - 1):
                    todo.append(lambda: v_y1(k - 1))
                if k == NU:
                    todo.append(lambda: v_out(NU - 1))
                if has(k + 1):
                    todo.append(lambda: v_qa(k + 1))
                if k == 0:
                    todo.append(lambda: small_d(0, 1))
                if k == 2:
                    todo.append(lambda: small_r(1, J))
                if k == 3:
                    todo.append(lambda: small_d(1, J))
                if k == 4:
                    todo.append(lambda: small_b(0, J))
                if has(k) and UNITS[k][1] == sum(SIZES[UNITS[k][0]][:5]):
                    todo.append(lambda: v_last(UNITS[k][0]))
                slots = len(todo)
                done = 0
                for m in range(slots):
                    todo[m]()
                    while done < len(pend) * (m + 1) // slots:
                        pend[done]()
                        done += 1
                for task in pend[done:]:
                    task()
                if has(k):
                    v_t2(k)
                pend = new

                load("A", k + 5)
                load("B", k + 4)
                load("C", k + 3)
                for g in w2_at.get(k + 1, []):
                    load_w2(g)
                if k == 0:
                    nc.sync.dma_start(out=w1r[:], in_=W1)
                    nc.sync.dma_start(out=cdr[:], in_=rows(cond))
                if k == 10:
                    for j, name in enumerate(("dn", "sg", "om", "tt")):
                        z1t = keep.tile([P, J, DIM], F32, name=name)
                        tiles["z1", j] = z1t[:].rearrange("p a d -> p (a d)")
                        nc.sync.dma_start(out=tiles["z1", j], in_=rows(z1)[:, j, :])

                for j in range(J):
                    if stage.get(j) == (k - 1, "turn"):
                        dz_mx(j)
                        stage[j] = (k, "mx")
                now = [(j, s) for j, s in mx_ready[:ready_now] if slot_pass[j, s] in w2_done[:w2_now]]
                now = [(j, s) for j, s in now if j < 2 or stage.get(j - 2, (0, ""))[1] == "store"][:MX_A_STEP]
                for j, s in now:
                    mx_ready.remove((j, s))
                    if mx(j, s):
                        pend.append(lambda j=j: dz_mask(j))
                        stage[j] = (k + 1, "mask")

            for task in pend:
                task()
            tail = [turn_dp(J - 1, group, "vector" if n % 2 else "scalar") for n, group in enumerate(groups[NU - 1])]
            for j, s in mx_ready:
                mx(j, s)
            mx_ready.clear()
            for task in tail:
                task()
            for j, s in mx_ready:
                mx(j, s)
            for j in range(J - 1):
                if stage[j][1] == "mask":
                    dz_turn(j)()
                if stage[j][1] in ("mask", "turn"):
                    dz_mx(j)
                if stage[j][1] != "store":
                    dz_store(j)
            dz_mask(J - 1)
            last_quant = dz_turn(J - 1)
            cut = 320
            dzi = keep.tile([P, HID, J], BF16, name="ea", align_bytes=64)
            nc.vector.tensor_copy(dzi[:, :cut, :], dz[:, :, :cut].rearrange("p j h -> p h j"))
            nc.scalar.copy(dzi[:, cut:, :], dz[:, :, cut:].rearrange("p j h -> p h j"))
            last_quant()
            nc.vector.quantize_mx(out=dziq[:].bitcast(E5M2), scales=dzis[:], in_=dzi[:].rearrange("p h j -> p (h j)"))
            dz_mx(J - 1)
            o1 = psum.tile([P, HID], F32, name="acc", bufs=2)
            nc.tensor.matmul_mx(out=o1[:], lhsT=cdq[:].bitcast(E4M3), lhsT_scale=cds[:], rhs=dziq[:].bitcast(E5M2), rhs_scale=dzis[:], start=True, stop=True)
            dz_store(J - 1)
            ob1 = work.tile([P, HID], F32, name="ob1", bufs=1)
            nc.scalar.copy(ob1[:], o1[:])
            nc.sync.dma_start(out=out_1, in_=ob1[:])
